import numpy as np
import ml_dtypes


def mxq(x, axis, fmt="e4m3"):
    dtype, down = {"e4m3": (ml_dtypes.float8_e4m3fn, 7), "e5m2": (ml_dtypes.float8_e5m2, 14)}[fmt]
    v = np.moveaxis(np.asarray(x, np.float32).astype(ml_dtypes.bfloat16).astype(np.float64), axis, -1)
    blocks = v.reshape(v.shape[:-1] + (-1, 32))
    amax = np.abs(blocks).max(-1, keepdims=True)
    byte = np.maximum(np.where(amax > 0, np.frexp(amax)[1] - 1 + 127, 0) - down, 1)
    scale = np.exp2(byte - 127.0)
    codes = (blocks / scale).astype(np.float32).astype(dtype).astype(np.float64)
    return np.moveaxis((codes * scale).reshape(v.shape), -1, axis)


WIDE = False


def mx_kscale(k):
    if not WIDE:
        return np.ones(k)
    levels = np.array([10, -10, 5, -5, 0])
    if k % 512:
        return np.exp2(np.random.permutation(np.resize(levels, k // 32))).repeat(32)
    a = np.empty((k // 512, 16))
    for p in range(k // 512):
        a[p, :8] = np.random.permutation(np.resize(levels, 8))
        for g in range(8):
            far = levels[np.abs(levels - a[p, g]) >= 10]
            a[p, g + 8] = far[np.random.randint(len(far))]
    return np.exp2(a.ravel()).repeat(32)


BF16 = ml_dtypes.bfloat16


def bf(x):
    return np.asarray(x, np.float32).astype(BF16)


def f64(x):
    return np.asarray(x).astype(np.float64)


B, IN, OUT, NK, DEG = 2048, 1024, 128, 10, 3
K0 = NK + DEG
JIT = 0.25


def b_spline_basis(x, t, degree):
    n0 = t.shape[0] - 1
    xe = x[..., None]
    basis = ((xe >= t[:-1]) & (xe < t[1:])).astype(np.float64)
    for p in range(1, degree + 1):
        ti = t[: n0 - p]
        tip = t[p:n0]
        ti1 = t[1 : n0 - p + 1]
        tip1 = t[p + 1 : n0 + 1]
        d1 = np.where(tip - ti > 0, tip - ti, np.ones_like(ti))
        d2 = np.where(tip1 - ti1 > 0, tip1 - ti1, np.ones_like(ti1))
        left = np.where(tip - ti > 0, (xe - ti) / d1, 0.0) * basis[..., : n0 - p]
        right = np.where(tip1 - ti1 > 0, (tip1 - xe) / d2, 0.0) * basis[..., 1 : n0 - p + 1]
        new = left + right
        pad = np.zeros(x.shape + (p,))
        basis = np.concatenate([new, pad], axis=-1)
    return basis


def setup_inputs():
    knots = np.linspace(0.0, 1.0, K0 + 1)
    knots[1:-1] += np.random.uniform(-JIT, JIT, K0 - 1) / K0
    s = mx_kscale(NK * IN)[:IN]
    g0 = np.exp2(np.round(np.log2((1.0 - JIT) / K0) - 0.5))
    c0 = np.exp2(np.round(np.log2(np.prod(np.arange(1, DEG + 1) / K0)) + 0.5))
    g = np.where(s < 1.0, g0 * s, 1.0)
    h = np.where(s < 1.0, c0 / g**DEG, 1.0)
    x = np.random.uniform(0.0, 1.0, (B, IN)) * g[None, :]
    cp = np.random.standard_normal((OUT, IN, K0)) * 1.5 / np.sqrt(IN)
    cp[:, :, 0] *= h[None, :]
    return {"x": bf(x), "knots": bf(knots), "control_points": bf(cp)}


def reference(x, knots, control_points):
    basis = b_spline_basis(f64(x), f64(knots), DEG)
    a = basis[:, :, :NK].transpose(0, 2, 1).reshape(B, NK * IN)
    w = f64(control_points)[:, :, :NK].transpose(2, 1, 0).reshape(NK * IN, OUT)
    return mxq(a, 1, "e4m3") @ mxq(w, 0, "e4m3")

@@ -1,0 +1,232 @@
+from contextlib import ExitStack
+
+import concourse.mybir as mybir
+from concourse.masks import make_identity
+
+F32 = mybir.dt.float32
+BF16 = mybir.dt.bfloat16
+U32 = mybir.dt.uint32
+U8 = mybir.dt.uint8
+FP8X4 = mybir.dt.float8_e4m3fn_x4
+ALU = mybir.AluOpType
+ACT = mybir.ActivationFunctionType
+
+P = 128
+PACK = 4
+BATCH = 2048
+FEATURES = 1024
+OUTPUTS = 128
+KNOTS = 14
+POINTS = 13
+BASES = 10
+HALVES = FEATURES // (P * PACK)
+ROWS = 512
+ROW_TILES = ROWS // P
+ROUNDS = BATCH // ROWS
+CHUNK = ROWS * PACK
+
+
+def feature_columns(n):
+    g, t = divmod(n, PACK)
+    return slice(g * P * PACK + t, (g + 1) * P * PACK, PACK)
+
+
+FLOPS = 2 * BATCH * BASES * FEATURES * OUTPUTS
+
+
+def spline_constants(nc, pool, knots):
+    knots_bf = pool.tile([P, KNOTS], BF16)
+    nc.sync.dma_start(out=knots_bf[:], in_=knots.partition_broadcast(P))
+    t = pool.tile([P, KNOTS], F32)
+    nc.vector.tensor_copy(out=t[:], in_=knots_bf[:])
+    neg_t = pool.tile([P, KNOTS], F32)
+    nc.vector.tensor_scalar_mul(out=neg_t[:], in0=t[:], scalar1=-1.0)
+
+    d1 = pool.tile([P, KNOTS - 1], F32)
+    d2 = pool.tile([P, KNOTS - 2], F32)
+    d3 = pool.tile([P, KNOTS - 3], F32)
+    d4 = pool.tile([P, KNOTS - 4], F32)
+    for step, diff in ((1, d1), (2, d2), (3, d3), (4, d4)):
+        nc.vector.tensor_sub(out=diff[:], in0=t[:, step:KNOTS], in1=t[:, 0 : KNOTS - step])
+
+    cubes = KNOTS - 3
+    p_prod = pool.tile([P, cubes], F32)
+    nc.vector.tensor_mul(out=p_prod[:], in0=d1[:, 0:cubes], in1=d2[:, 0:cubes])
+    nc.vector.tensor_mul(out=p_prod[:], in0=p_prod[:], in1=d3[:, 0:cubes])
+    p_scale = pool.tile([P, cubes], F32)
+    nc.vector.reciprocal(out=p_scale[:], in_=p_prod[:])
+    q_prod = pool.tile([P, cubes], F32)
+    nc.vector.tensor_mul(out=q_prod[:], in0=d1[:, 2 : 2 + cubes], in1=d2[:, 1 : 1 + cubes])
+    nc.vector.tensor_mul(out=q_prod[:], in0=q_prod[:], in1=d3[:, 0:cubes])
+    q_recip = pool.tile([P, cubes], F32)
+    nc.vector.reciprocal(out=q_recip[:], in_=q_prod[:])
+    q_scale = pool.tile([P, cubes], F32)
+    nc.vector.tensor_scalar_mul(out=q_scale[:], in0=q_recip[:], scalar1=-1.0)
+
+    d1_recip = pool.tile([P, KNOTS - 1], F32)
+    nc.vector.reciprocal(out=d1_recip[:], in_=d1[:])
+    neg_d4 = pool.tile([P, BASES], F32)
+    nc.vector.tensor_scalar_mul(out=neg_d4[:], in0=d4[:], scalar1=-1.0)
+    left_w = pool.tile([P, BASES], F32)
+    nc.vector.tensor_mul(out=left_w[:], in0=neg_d4[:], in1=d1_recip[:, 0:BASES])
+    right_w = pool.tile([P, BASES], F32)
+    nc.vector.tensor_mul(out=right_w[:], in0=neg_d4[:], in1=d1_recip[:, 3 : 3 + BASES])
+    return {
+        "t": t,
+        "neg_t": neg_t,
+        "p_scale": p_scale,
+        "q_scale": q_scale,
+        "left_w": left_w,
+        "right_w": right_w,
+    }
+
+
+def tile_kanlayer_kernel(tc, x, knots, control_points, out):
+    nc = tc.nc
+    with ExitStack() as ctx:
+        consts = ctx.enter_context(tc.tile_pool(name="consts", bufs=1))
+        weights = ctx.enter_context(tc.tile_pool(name="weights", bufs=1))
+        stage = ctx.enter_context(tc.tile_pool(name="stage", bufs=2))
+        x_pool = ctx.enter_context(tc.tile_pool(name="x_pool", bufs=ROW_TILES))
+        cube_pool = ctx.enter_context(tc.tile_pool(name="cube_pool", bufs=3))
+        left_pool = ctx.enter_context(tc.tile_pool(name="left_pool", bufs=6))
+        mx_pool = ctx.enter_context(tc.tile_pool(name="mx_pool", bufs=3))
+        flip_psum = ctx.enter_context(tc.psum_pool(name="flip_psum", bufs=3))
+        acc_psum = ctx.enter_context(tc.psum_pool(name="acc_psum", bufs=1))
+
+        ident = consts.tile([P, P], BF16)
+        make_identity(nc, ident[:])
+        c = spline_constants(nc, consts, knots)
+
+        def load_rows(r):
+            tiles = []
+            for m in range(ROW_TILES):
+                x_sb = x_pool.tile([P, FEATURES], BF16, name="x_sb")
+                first = r * ROWS + m * P
+                nc.sync.dma_start(out=x_sb[:], in_=x[first : first + P, :])
+                tiles.append(x_sb)
+            return tiles
+
+        x_first = load_rows(0)
+
+        cp_sb = weights.tile([P, FEATURES, POINTS], BF16)
+        nc.sync.dma_start(out=cp_sb[:], in_=control_points)
+        w_codes = weights.tile([P, BASES, HALVES * OUTPUTS], U32, align_bytes=64)
+        w_scales = weights.tile([P, BASES, HALVES * OUTPUTS], U8, align_bytes=64)
+        for k in range(BASES):
+            w_flip = flip_psum.tile([P, HALVES * PACK, P], BF16, name="flip")
+            for n in range(HALVES * PACK):
+                nc.tensor.transpose(w_flip[:, n, :], cp_sb[:, feature_columns(n), k], ident[:])
+            w_grouped = stage.tile([P, HALVES, OUTPUTS, PACK], BF16, align_bytes=64)
+            nc.scalar.copy(
+                out=w_grouped[:], in_=w_flip[:].rearrange("p (g t) o -> p g o t", g=HALVES)
+            )
+            nc.vector.quantize_mx(
+                out=w_codes[:, k, :].bitcast(FP8X4),
+                scales=w_scales[:, k, :],
+                in_=w_grouped[:].rearrange("p g o t -> p (g o t)"),
+            )
+
+        for r in range(ROUNDS):
+            x_tiles = x_first if r == 0 else load_rows(r)
+            v = stage.tile([P, HALVES, ROWS, PACK], BF16)
+            for m in range(ROW_TILES):
+                x_flip = flip_psum.tile([P, HALVES * PACK, P], BF16, name="flip")
+                for n in range(HALVES * PACK):
+                    nc.tensor.transpose(
+                        x_flip[:, n, :], x_tiles[m][:, feature_columns(n)], ident[:]
+                    )
+                nc.scalar.copy(
+                    out=v[:, :, m * P : (m + 1) * P, :],
+                    in_=x_flip[:].rearrange("p (g t) b -> p g b t", g=HALVES),
+                )
+
+            acc = [
+                acc_psum.tile([P, OUTPUTS], F32, name="acc%d" % m) for m in range(ROW_TILES)
+            ]
+            for g in range(HALVES):
+                vg = v[:, g, :, :].rearrange("p b t -> p (b t)")
+                p_cube = {}
+                q_cube = {}
+                left = {}
+                for i in range(KNOTS):
+                    square = cube_pool.tile([P, CHUNK], F32)
+                    nc.scalar.activation(
+                        out=square[:], in_=vg, func=ACT.Square, bias=c["neg_t"][:, i : i + 1]
+                    )
+                    cube = cube_pool.tile([P, CHUNK], F32)
+                    nc.vector.scalar_tensor_tensor(
+                        out=cube[:],
+                        in0=vg,
+                        scalar=c["t"][:, i : i + 1],
+                        in1=square[:],
+                        op0=ALU.subtract,
+                        op1=ALU.mult,
+                    )
+                    if i <= KNOTS - 4:
+                        p_cube[i] = cube_pool.tile([P, CHUNK], F32, name="p_cube")
+                        nc.scalar.activation(
+                            out=p_cube[i][:],
+                            in_=cube[:],
+                            func=ACT.Relu,
+                            scale=c["p_scale"][:, i : i + 1],
+                        )
+                    if i >= 3:
+                        q_cube[i] = cube_pool.tile([P, CHUNK], F32, name="q_cube")
+                        nc.scalar.activation(
+                            out=q_cube[i][:],
+                            in_=cube[:],
+                            func=ACT.Relu,
+                            scale=c["q_scale"][:, i - 3 : i - 2],
+                        )
+                    if 1 <= i <= BASES:
+                        k = i - 1
+                        left[k] = left_pool.tile([P, CHUNK], BF16, name="left")
+                        nc.vector.scalar_tensor_tensor(
+                            out=left[k][:],
+                            in0=p_cube[k + 1][:],
+                            scalar=c["left_w"][:, k : k + 1],
+                            in1=p_cube[k][:],
+                            op0=ALU.mult,
+                            op1=ALU.add,
+                        )
+                    if i >= 4:
+                        k = i - 4
+                        right = stage.tile([P, CHUNK], BF16)
+                        nc.vector.scalar_tensor_tensor(
+                            out=right[:],
+                            in0=q_cube[k + 3][:],
+                            scalar=c["right_w"][:, k : k + 1],
+                            in1=q_cube[k + 4][:],
+                            op0=ALU.mult,
+                            op1=ALU.add,
+                        )
+                        basis = mx_pool.tile([P, CHUNK], BF16, align_bytes=64)
+                        nc.vector.tensor_tensor(
+                            out=basis[:], in0=left[k][:], in1=right[:], op=ALU.max
+                        )
+                        b_codes = mx_pool.tile([P, ROWS], U32, align_bytes=64)
+                        b_scales = mx_pool.tile([P, ROWS], U8, align_bytes=64)
+                        nc.vector.quantize_mx(
+                            out=b_codes[:].bitcast(FP8X4), scales=b_scales[:], in_=basis[:]
+                        )
+                        o_cols = slice(g * OUTPUTS, (g + 1) * OUTPUTS)
+                        for m in range(ROW_TILES):
+                            b_cols = slice(m * P, (m + 1) * P)
+                            nc.tensor.matmul_mx(
+                                out=acc[m][:],
+                                lhsT=b_codes[:, b_cols].bitcast(FP8X4),
+                                lhsT_scale=b_scales[:, b_cols],
+                                rhs=w_codes[:, k, o_cols].bitcast(FP8X4),
+                                rhs_scale=w_scales[:, k, o_cols],
+                                start=(g == 0 and k == 0),
+                                stop=(g == HALVES - 1 and k == BASES - 1),
+                            )
+
+            result = stage.tile([P, ROW_TILES, OUTPUTS], F32)
+            for m in range(ROW_TILES):
+                nc.scalar.copy(out=result[:, m, :], in_=acc[m][:])
+            nc.sync.dma_start(
+                out=out[r * ROWS : (r + 1) * ROWS, :].rearrange("(m p) o -> p m o", p=P),
+                in_=result[:],
+            )

@@ -24,14 +24,18 @@ ROWS = 512
 ROW_TILES = ROWS // P
 ROUNDS = BATCH // ROWS
 CHUNK = ROWS * PACK
+TINY = 2.0**-60
+
+P_ONLY = (0, 1, 2)
+BOTH = (3, 4, 5, 6, 7, 8, 9, 10)
+Q_ONLY = (11, 12, 13)
+
+FLOPS = 2 * BATCH * BASES * FEATURES * OUTPUTS
 
 
 def feature_columns(n):
     g, t = divmod(n, PACK)
     return slice(g * P * PACK + t, (g + 1) * P * PACK, PACK)
-
-
-FLOPS = 2 * BATCH * BASES * FEATURES * OUTPUTS
 
 
 def spline_constants(nc, pool, knots):
@@ -41,6 +45,8 @@ def spline_constants(nc, pool, knots):
     nc.vector.tensor_copy(out=t[:], in_=knots_bf[:])
     neg_t = pool.tile([P, KNOTS], F32)
     nc.vector.tensor_scalar_mul(out=neg_t[:], in0=t[:], scalar1=-1.0)
+    first_bias = pool.tile([P, 1], F32)
+    nc.vector.tensor_scalar_add(out=first_bias[:], in0=neg_t[:, 0:1], scalar1=TINY)
 
     d1 = pool.tile([P, KNOTS - 1], F32)
     d2 = pool.tile([P, KNOTS - 2], F32)
@@ -62,6 +68,10 @@ def spline_constants(nc, pool, knots):
     nc.vector.reciprocal(out=q_recip[:], in_=q_prod[:])
     q_scale = pool.tile([P, cubes], F32)
     nc.vector.tensor_scalar_mul(out=q_scale[:], in0=q_recip[:], scalar1=-1.0)
+    p_log = pool.tile([P, cubes], F32)
+    nc.scalar.activation(out=p_log[:], in_=p_scale[:], func=ACT.Ln)
+    q_log = pool.tile([P, cubes], F32)
+    nc.scalar.activation(out=q_log[:], in_=q_recip[:], func=ACT.Ln)
 
     d1_recip = pool.tile([P, KNOTS - 1], F32)
     nc.vector.reciprocal(out=d1_recip[:], in_=d1[:])
@@ -74,8 +84,11 @@ def spline_constants(nc, pool, knots):
     return {
         "t": t,
         "neg_t": neg_t,
+        "first_bias": first_bias,
         "p_scale": p_scale,
         "q_scale": q_scale,
+        "p_log": p_log,
+        "q_log": q_log,
         "left_w": left_w,
         "right_w": right_w,
     }
@@ -86,17 +99,13 @@ def tile_kanlayer_kernel(tc, x, knots, control_points, out):
     with ExitStack() as ctx:
         consts = ctx.enter_context(tc.tile_pool(name="consts", bufs=1))
         weights = ctx.enter_context(tc.tile_pool(name="weights", bufs=1))
-        stage = ctx.enter_context(tc.tile_pool(name="stage", bufs=2))
         x_pool = ctx.enter_context(tc.tile_pool(name="x_pool", bufs=ROW_TILES))
-        cube_pool = ctx.enter_context(tc.tile_pool(name="cube_pool", bufs=3))
-        left_pool = ctx.enter_context(tc.tile_pool(name="left_pool", bufs=6))
-        mx_pool = ctx.enter_context(tc.tile_pool(name="mx_pool", bufs=3))
+        v_pool = ctx.enter_context(tc.tile_pool(name="v_pool", bufs=2))
         flip_psum = ctx.enter_context(tc.psum_pool(name="flip_psum", bufs=3))
         acc_psum = ctx.enter_context(tc.psum_pool(name="acc_psum", bufs=1))
 
         ident = consts.tile([P, P], BF16)
         make_identity(nc, ident[:])
-        c = spline_constants(nc, consts, knots)
 
         def load_rows(r):
             tiles = []
@@ -107,29 +116,8 @@ def tile_kanlayer_kernel(tc, x, knots, control_points, out):
                 tiles.append(x_sb)
             return tiles
 
-        x_first = load_rows(0)
-
-        cp_sb = weights.tile([P, FEATURES, POINTS], BF16)
-        nc.sync.dma_start(out=cp_sb[:], in_=control_points)
-        w_codes = weights.tile([P, BASES, HALVES * OUTPUTS], U32, align_bytes=64)
-        w_scales = weights.tile([P, BASES, HALVES * OUTPUTS], U8, align_bytes=64)
-        for k in range(BASES):
-            w_flip = flip_psum.tile([P, HALVES * PACK, P], BF16, name="flip")
-            for n in range(HALVES * PACK):
-                nc.tensor.transpose(w_flip[:, n, :], cp_sb[:, feature_columns(n), k], ident[:])
-            w_grouped = stage.tile([P, HALVES, OUTPUTS, PACK], BF16, align_bytes=64)
-            nc.scalar.copy(
-                out=w_grouped[:], in_=w_flip[:].rearrange("p (g t) o -> p g o t", g=HALVES)
-            )
-            nc.vector.quantize_mx(
-                out=w_codes[:, k, :].bitcast(FP8X4),
-                scales=w_scales[:, k, :],
-                in_=w_grouped[:].rearrange("p g o t -> p (g o t)"),
-            )
-
-        for r in range(ROUNDS):
-            x_tiles = x_first if r == 0 else load_rows(r)
-            v = stage.tile([P, HALVES, ROWS, PACK], BF16)
+        def flip_rows(x_tiles):
+            v = v_pool.tile([P, HALVES, ROWS, PACK], BF16, name="v")
             for m in range(ROW_TILES):
                 x_flip = flip_psum.tile([P, HALVES * PACK, P], BF16, name="flip")
                 for n in range(HALVES * PACK):
@@ -140,90 +128,180 @@ def tile_kanlayer_kernel(tc, x, knots, control_points, out):
                     out=v[:, :, m * P : (m + 1) * P, :],
                     in_=x_flip[:].rearrange("p (g t) b -> p g b t", g=HALVES),
                 )
+            return v
 
-            acc = [
-                acc_psum.tile([P, OUTPUTS], F32, name="acc%d" % m) for m in range(ROW_TILES)
-            ]
+        c = spline_constants(nc, consts, knots)
+        v_now = flip_rows(load_rows(0))
+
+        w_codes = weights.tile([P, BASES, HALVES * OUTPUTS], U32, align_bytes=64)
+        w_scales = weights.tile([P, BASES, HALVES * OUTPUTS], U8, align_bytes=64)
+        with tc.tile_pool(name="cp_pool", bufs=1) as cp_pool:
+            cp_sb = cp_pool.tile([P, FEATURES, POINTS], BF16, name="cp_sb")
+            nc.sync.dma_start(out=cp_sb[:], in_=control_points)
+            for k in range(BASES):
+                w_flip = flip_psum.tile([P, HALVES * PACK, P], BF16, name="flip")
+                for n in range(HALVES * PACK):
+                    nc.tensor.transpose(w_flip[:, n, :], cp_sb[:, feature_columns(n), k], ident[:])
+                w_grouped = cp_pool.tile(
+                    [P, HALVES, OUTPUTS, PACK], BF16, name="w_grouped%d" % (k % 2), align_bytes=64
+                )
+                nc.vector.tensor_copy(
+                    out=w_grouped[:], in_=w_flip[:].rearrange("p (g t) o -> p g o t", g=HALVES)
+                )
+                nc.vector.quantize_mx(
+                    out=w_codes[:, k, :].bitcast(FP8X4),
+                    scales=w_scales[:, k, :],
+                    in_=w_grouped[:].rearrange("p g o t -> p (g o t)"),
+                )
+
+        stage = ctx.enter_context(tc.tile_pool(name="stage", bufs=2))
+        single_pool = ctx.enter_context(tc.tile_pool(name="single_pool", bufs=1))
+        cube_pool = ctx.enter_context(tc.tile_pool(name="cube_pool", bufs=2))
+        side_pool = ctx.enter_context(tc.tile_pool(name="side_pool", bufs=3))
+        left_pool = ctx.enter_context(tc.tile_pool(name="left_pool", bufs=6))
+        mx_pool = ctx.enter_context(tc.tile_pool(name="mx_pool", bufs=2))
+
+        def single_log(vg, i):
+            log = single_pool.tile([P, CHUNK], F32, name="single%d" % i)
+            if i == 0:
+                nc.scalar.activation(out=log[:], in_=vg, func=ACT.Ln, bias=c["first_bias"][:])
+                return log
+            on_right = i in P_ONLY
+            nc.vector.tensor_scalar(
+                out=log[:],
+                in0=vg,
+                scalar1=c["t"][:, i : i + 1],
+                scalar2=TINY if on_right else -TINY,
+                op0=ALU.subtract,
+                op1=ALU.max if on_right else ALU.min,
+            )
+            nc.scalar.activation(
+                out=log[:], in_=log[:], func=ACT.Ln, scale=1.0 if on_right else -1.0
+            )
+            return log
+
+        def single_exp(log, i):
+            factor = c["p_log"][:, i : i + 1] if i in P_ONLY else c["q_log"][:, i - 3 : i - 2]
+            nc.scalar.activation(out=log[:], in_=log[:], func=ACT.Exp, scale=3.0, bias=factor)
+            return log
+
+        def signed_cube(vg, i):
+            square = cube_pool.tile([P, CHUNK], F32, name="square")
+            nc.scalar.activation(
+                out=square[:], in_=vg, func=ACT.Square, bias=c["neg_t"][:, i : i + 1]
+            )
+            cube = cube_pool.tile([P, CHUNK], F32, name="cube")
+            nc.vector.scalar_tensor_tensor(
+                out=cube[:],
+                in0=vg,
+                scalar=c["t"][:, i : i + 1],
+                in1=square[:],
+                op0=ALU.subtract,
+                op1=ALU.mult,
+            )
+            return cube
+
+        def both_sides(cube, i):
+            p_cube = side_pool.tile([P, CHUNK], F32, name="p_cube")
+            nc.scalar.activation(
+                out=p_cube[:], in_=cube[:], func=ACT.Relu, scale=c["p_scale"][:, i : i + 1]
+            )
+            q_cube = side_pool.tile([P, CHUNK], F32, name="q_cube")
+            nc.scalar.activation(
+                out=q_cube[:], in_=cube[:], func=ACT.Relu, scale=c["q_scale"][:, i - 3 : i - 2]
+            )
+            return p_cube, q_cube
+
+        def left_side(k, p_cube):
+            left = left_pool.tile([P, CHUNK], BF16, name="left")
+            nc.vector.scalar_tensor_tensor(
+                out=left[:],
+                in0=p_cube[k + 1][:],
+                scalar=c["left_w"][:, k : k + 1],
+                in1=p_cube[k][:],
+                op0=ALU.mult,
+                op1=ALU.add,
+            )
+            return left
+
+        def basis_function(k, left, q_cube, g, acc):
+            right = stage.tile([P, CHUNK], BF16, name="right")
+            nc.vector.scalar_tensor_tensor(
+                out=right[:],
+                in0=q_cube[k + 3][:],
+                scalar=c["right_w"][:, k : k + 1],
+                in1=q_cube[k + 4][:],
+                op0=ALU.mult,
+                op1=ALU.add,
+            )
+            basis = mx_pool.tile([P, CHUNK], BF16, name="basis", align_bytes=64)
+            nc.vector.tensor_tensor(out=basis[:], in0=left[:], in1=right[:], op=ALU.max)
+            b_codes = mx_pool.tile([P, ROWS], U32, name="b_codes", align_bytes=64)
+            b_scales = mx_pool.tile([P, ROWS], U8, name="b_scales", align_bytes=64)
+            nc.vector.quantize_mx(
+                out=b_codes[:].bitcast(FP8X4), scales=b_scales[:], in_=basis[:]
+            )
+            o_cols = slice(g * OUTPUTS, (g + 1) * OUTPUTS)
+            for m in range(ROW_TILES):
+                b_cols = slice(m * P, (m + 1) * P)
+                nc.tensor.matmul_mx(
+                    out=acc[m][:],
+                    lhsT=b_codes[:, b_cols].bitcast(FP8X4),
+                    lhsT_scale=b_scales[:, b_cols],
+                    rhs=w_codes[:, k, o_cols].bitcast(FP8X4),
+                    rhs_scale=w_scales[:, k, o_cols],
+                    start=(g == 0 and k == 0),
+                    stop=(g == HALVES - 1 and k == BASES - 1),
+                )
+
+        def values(v, g):
+            return v[:, g, :, :].rearrange("p b t -> p (b t)")
+
+        p_next = {i: single_log(values(v_now, 0), i) for i in P_ONLY}
+        for i in P_ONLY:
+            single_exp(p_next[i], i)
+        sides_next = both_sides(signed_cube(values(v_now, 0), BOTH[0]), BOTH[0])
+
+        for r in range(ROUNDS):
+            acc = [acc_psum.tile([P, OUTPUTS], F32, name="acc%d" % m) for m in range(ROW_TILES)]
             for g in range(HALVES):
-                vg = v[:, g, :, :].rearrange("p b t -> p (b t)")
-                p_cube = {}
+                last = r == ROUNDS - 1 and g == HALVES - 1
+                vg = values(v_now, g)
+                if g == HALVES - 1 and not last:
+                    v_now = flip_rows(x_tiles)
+                elif not last and r < ROUNDS - 1:
+                    x_tiles = load_rows(r + 1)
+                v_after = None if last else values(v_now, (g + 1) % HALVES)
+
+                p_cube = dict(p_next)
+                p_next = {}
                 q_cube = {}
                 left = {}
-                for i in range(KNOTS):
-                    square = cube_pool.tile([P, CHUNK], F32)
-                    nc.scalar.activation(
-                        out=square[:], in_=vg, func=ACT.Square, bias=c["neg_t"][:, i : i + 1]
-                    )
-                    cube = cube_pool.tile([P, CHUNK], F32)
-                    nc.vector.scalar_tensor_tensor(
-                        out=cube[:],
-                        in0=vg,
-                        scalar=c["t"][:, i : i + 1],
-                        in1=square[:],
-                        op0=ALU.subtract,
-                        op1=ALU.mult,
-                    )
-                    if i <= KNOTS - 4:
-                        p_cube[i] = cube_pool.tile([P, CHUNK], F32, name="p_cube")
-                        nc.scalar.activation(
-                            out=p_cube[i][:],
-                            in_=cube[:],
-                            func=ACT.Relu,
-                            scale=c["p_scale"][:, i : i + 1],
-                        )
-                    if i >= 3:
-                        q_cube[i] = cube_pool.tile([P, CHUNK], F32, name="q_cube")
-                        nc.scalar.activation(
-                            out=q_cube[i][:],
-                            in_=cube[:],
-                            func=ACT.Relu,
-                            scale=c["q_scale"][:, i - 3 : i - 2],
-                        )
-                    if 1 <= i <= BASES:
-                        k = i - 1
-                        left[k] = left_pool.tile([P, CHUNK], BF16, name="left")
-                        nc.vector.scalar_tensor_tensor(
-                            out=left[k][:],
-                            in0=p_cube[k + 1][:],
-                            scalar=c["left_w"][:, k : k + 1],
-                            in1=p_cube[k][:],
-                            op0=ALU.mult,
-                            op1=ALU.add,
-                        )
-                    if i >= 4:
-                        k = i - 4
-                        right = stage.tile([P, CHUNK], BF16)
-                        nc.vector.scalar_tensor_tensor(
-                            out=right[:],
-                            in0=q_cube[k + 3][:],
-                            scalar=c["right_w"][:, k : k + 1],
-                            in1=q_cube[k + 4][:],
-                            op0=ALU.mult,
-                            op1=ALU.add,
-                        )
-                        basis = mx_pool.tile([P, CHUNK], BF16, align_bytes=64)
-                        nc.vector.tensor_tensor(
-                            out=basis[:], in0=left[k][:], in1=right[:], op=ALU.max
-                        )
-                        b_codes = mx_pool.tile([P, ROWS], U32, align_bytes=64)
-                        b_scales = mx_pool.tile([P, ROWS], U8, align_bytes=64)
-                        nc.vector.quantize_mx(
-                            out=b_codes[:].bitcast(FP8X4), scales=b_scales[:], in_=basis[:]
-                        )
-                        o_cols = slice(g * OUTPUTS, (g + 1) * OUTPUTS)
-                        for m in range(ROW_TILES):
-                            b_cols = slice(m * P, (m + 1) * P)
-                            nc.tensor.matmul_mx(
-                                out=acc[m][:],
-                                lhsT=b_codes[:, b_cols].bitcast(FP8X4),
-                                lhsT_scale=b_scales[:, b_cols],
-                                rhs=w_codes[:, k, o_cols].bitcast(FP8X4),
-                                rhs_scale=w_scales[:, k, o_cols],
-                                start=(g == 0 and k == 0),
-                                stop=(g == HALVES - 1 and k == BASES - 1),
-                            )
+                for i in BOTH:
+                    p_cube[i], q_cube[i] = sides_next
+                    if i < BOTH[-1]:
+                        sides_next = both_sides(signed_cube(vg, i + 1), i + 1)
+                    elif not last:
+                        sides_next = both_sides(signed_cube(v_after, BOTH[0]), BOTH[0])
 
-            result = stage.tile([P, ROW_TILES, OUTPUTS], F32)
+                    if 3 <= i <= 5:
+                        q_cube[i + 8] = single_log(vg, i + 8)
+                    if 6 <= i <= 8 and not last:
+                        p_next[i - 6] = single_log(v_after, i - 6)
+                    if i == 9:
+                        single_exp(q_cube[11], 11)
+                        single_exp(q_cube[12], 12)
+                    if i == 10:
+                        single_exp(q_cube[13], 13)
+                        for n in sorted(p_next):
+                            single_exp(p_next[n], n)
+
+                    for k in (0, 1, 2) if i == 3 else (i - 1,):
+                        left[k] = left_side(k, p_cube)
+                    for k in () if i == 3 else (6, 7, 8, 9) if i == 10 else (i - 4,):
+                        basis_function(k, left[k], q_cube, g, acc)
+
+            result = stage.tile([P, ROW_TILES, OUTPUTS], F32, name="result")
             for m in range(ROW_TILES):
                 nc.scalar.copy(out=result[:, m, :], in_=acc[m][:])
             nc.sync.dma_start(

@@ -101,11 +101,15 @@ def tile_kanlayer_kernel(tc, x, knots, control_points, out):
         weights = ctx.enter_context(tc.tile_pool(name="weights", bufs=1))
         x_pool = ctx.enter_context(tc.tile_pool(name="x_pool", bufs=ROW_TILES))
         v_pool = ctx.enter_context(tc.tile_pool(name="v_pool", bufs=2))
+        stage = ctx.enter_context(tc.tile_pool(name="stage", bufs=2))
+        single_pool = ctx.enter_context(tc.tile_pool(name="single_pool", bufs=1))
+        cube_pool = ctx.enter_context(tc.tile_pool(name="cube_pool", bufs=2))
+        side_pool = ctx.enter_context(tc.tile_pool(name="side_pool", bufs=3))
+        left_pool = ctx.enter_context(tc.tile_pool(name="left_pool", bufs=6))
+        mx_pool = ctx.enter_context(tc.tile_pool(name="mx_pool", bufs=2))
         flip_psum = ctx.enter_context(tc.psum_pool(name="flip_psum", bufs=3))
         acc_psum = ctx.enter_context(tc.psum_pool(name="acc_psum", bufs=1))
-
-        ident = consts.tile([P, P], BF16)
-        make_identity(nc, ident[:])
+        ctx.enter_context(tc.manual_schedule(engines={mybir.EngineType.Activation}))
 
         def load_rows(r):
             tiles = []
@@ -115,6 +119,18 @@ def tile_kanlayer_kernel(tc, x, knots, control_points, out):
                 nc.sync.dma_start(out=x_sb[:], in_=x[first : first + P, :])
                 tiles.append(x_sb)
             return tiles
+
+        def load_points(g):
+            cp_sb = weights.tile([P, P * PACK, POINTS], BF16, name="cp_sb")
+            first = g * P * PACK
+            nc.sync.dma_start(out=cp_sb[:], in_=control_points[:, first : first + P * PACK, :])
+            return cp_sb
+
+        x_tiles = load_rows(0)
+        c = spline_constants(nc, consts, knots)
+        cp_sb = load_points(0)
+        ident = consts.tile([P, P], BF16)
+        make_identity(nc, ident[:])
 
         def flip_rows(x_tiles):
             v = v_pool.tile([P, HALVES, ROWS, PACK], BF16, name="v")
@@ -130,66 +146,55 @@ def tile_kanlayer_kernel(tc, x, knots, control_points, out):
                 )
             return v
 
-        c = spline_constants(nc, consts, knots)
-        v_now = flip_rows(load_rows(0))
-
         w_codes = weights.tile([P, BASES, HALVES * OUTPUTS], U32, align_bytes=64)
         w_scales = weights.tile([P, BASES, HALVES * OUTPUTS], U8, align_bytes=64)
-        with tc.tile_pool(name="cp_pool", bufs=1) as cp_pool:
-            cp_sb = cp_pool.tile([P, FEATURES, POINTS], BF16, name="cp_sb")
-            nc.sync.dma_start(out=cp_sb[:], in_=control_points)
-            for k in range(BASES):
-                w_flip = flip_psum.tile([P, HALVES * PACK, P], BF16, name="flip")
-                for n in range(HALVES * PACK):
-                    nc.tensor.transpose(w_flip[:, n, :], cp_sb[:, feature_columns(n), k], ident[:])
-                w_grouped = cp_pool.tile(
-                    [P, HALVES, OUTPUTS, PACK], BF16, name="w_grouped%d" % (k % 2), align_bytes=64
-                )
-                nc.vector.tensor_copy(
-                    out=w_grouped[:], in_=w_flip[:].rearrange("p (g t) o -> p g o t", g=HALVES)
-                )
-                nc.vector.quantize_mx(
-                    out=w_codes[:, k, :].bitcast(FP8X4),
-                    scales=w_scales[:, k, :],
-                    in_=w_grouped[:].rearrange("p g o t -> p (g o t)"),
-                )
 
-        stage = ctx.enter_context(tc.tile_pool(name="stage", bufs=2))
-        single_pool = ctx.enter_context(tc.tile_pool(name="single_pool", bufs=1))
-        cube_pool = ctx.enter_context(tc.tile_pool(name="cube_pool", bufs=2))
-        side_pool = ctx.enter_context(tc.tile_pool(name="side_pool", bufs=3))
-        left_pool = ctx.enter_context(tc.tile_pool(name="left_pool", bufs=6))
-        mx_pool = ctx.enter_context(tc.tile_pool(name="mx_pool", bufs=2))
+        def prepare_weights(cp_sb, g, k):
+            w_flip = flip_psum.tile([P, PACK, P], BF16, name="flip")
+            for t in range(PACK):
+                nc.tensor.transpose(w_flip[:, t, :], cp_sb[:, feature_columns(t), k], ident[:])
+            w_grouped = stage.tile([P, OUTPUTS, PACK], BF16, name="w_grouped", align_bytes=64)
+            nc.vector.tensor_copy(out=w_grouped[:], in_=w_flip[:].rearrange("p t o -> p o t"))
+            o_cols = slice(g * OUTPUTS, (g + 1) * OUTPUTS)
+            nc.vector.quantize_mx(
+                out=w_codes[:, k, o_cols].bitcast(FP8X4),
+                scales=w_scales[:, k, o_cols],
+                in_=w_grouped[:].rearrange("p o t -> p (o t)"),
+            )
 
-        def single_log(vg, i):
-            log = single_pool.tile([P, CHUNK], F32, name="single%d" % i)
+        def single_clamp(vg, i):
+            dist = single_pool.tile([P, CHUNK], F32, name="single%d" % i)
+            if i > 0:
+                on_right = i in P_ONLY
+                nc.vector.tensor_scalar(
+                    out=dist[:],
+                    in0=vg,
+                    scalar1=c["t"][:, i : i + 1],
+                    scalar2=TINY if on_right else -TINY,
+                    op0=ALU.subtract,
+                    op1=ALU.max if on_right else ALU.min,
+                )
+            return dist
+
+        def single_log(vg, i, dist):
             if i == 0:
-                nc.scalar.activation(out=log[:], in_=vg, func=ACT.Ln, bias=c["first_bias"][:])
-                return log
-            on_right = i in P_ONLY
-            nc.vector.tensor_scalar(
-                out=log[:],
-                in0=vg,
-                scalar1=c["t"][:, i : i + 1],
-                scalar2=TINY if on_right else -TINY,
-                op0=ALU.subtract,
-                op1=ALU.max if on_right else ALU.min,
-            )
-            nc.scalar.activation(
-                out=log[:], in_=log[:], func=ACT.Ln, scale=1.0 if on_right else -1.0
-            )
-            return log
+                nc.scalar.activation(out=dist[:], in_=vg, func=ACT.Ln, bias=c["first_bias"][:])
+            else:
+                sign = 1.0 if i in P_ONLY else -1.0
+                nc.scalar.activation(out=dist[:], in_=dist[:], func=ACT.Ln, scale=sign)
 
-        def single_exp(log, i):
+        def single_exp(i, log):
             factor = c["p_log"][:, i : i + 1] if i in P_ONLY else c["q_log"][:, i - 3 : i - 2]
             nc.scalar.activation(out=log[:], in_=log[:], func=ACT.Exp, scale=3.0, bias=factor)
-            return log
 
-        def signed_cube(vg, i):
+        def make_square(vg, i):
             square = cube_pool.tile([P, CHUNK], F32, name="square")
             nc.scalar.activation(
                 out=square[:], in_=vg, func=ACT.Square, bias=c["neg_t"][:, i : i + 1]
             )
+            return square
+
+        def signed_cube(vg, i, square):
             cube = cube_pool.tile([P, CHUNK], F32, name="cube")
             nc.vector.scalar_tensor_tensor(
                 out=cube[:],
@@ -257,50 +262,10 @@ def tile_kanlayer_kernel(tc, x, knots, control_points, out):
         def values(v, g):
             return v[:, g, :, :].rearrange("p b t -> p (b t)")
 
-        p_next = {i: single_log(values(v_now, 0), i) for i in P_ONLY}
-        for i in P_ONLY:
-            single_exp(p_next[i], i)
-        sides_next = both_sides(signed_cube(values(v_now, 0), BOTH[0]), BOTH[0])
+        def new_sums():
+            return [acc_psum.tile([P, OUTPUTS], F32, name="acc%d" % m) for m in range(ROW_TILES)]
 
-        for r in range(ROUNDS):
-            acc = [acc_psum.tile([P, OUTPUTS], F32, name="acc%d" % m) for m in range(ROW_TILES)]
-            for g in range(HALVES):
-                last = r == ROUNDS - 1 and g == HALVES - 1
-                vg = values(v_now, g)
-                if g == HALVES - 1 and not last:
-                    v_now = flip_rows(x_tiles)
-                elif not last and r < ROUNDS - 1:
-                    x_tiles = load_rows(r + 1)
-                v_after = None if last else values(v_now, (g + 1) % HALVES)
-
-                p_cube = dict(p_next)
-                p_next = {}
-                q_cube = {}
-                left = {}
-                for i in BOTH:
-                    p_cube[i], q_cube[i] = sides_next
-                    if i < BOTH[-1]:
-                        sides_next = both_sides(signed_cube(vg, i + 1), i + 1)
-                    elif not last:
-                        sides_next = both_sides(signed_cube(v_after, BOTH[0]), BOTH[0])
-
-                    if 3 <= i <= 5:
-                        q_cube[i + 8] = single_log(vg, i + 8)
-                    if 6 <= i <= 8 and not last:
-                        p_next[i - 6] = single_log(v_after, i - 6)
-                    if i == 9:
-                        single_exp(q_cube[11], 11)
-                        single_exp(q_cube[12], 12)
-                    if i == 10:
-                        single_exp(q_cube[13], 13)
-                        for n in sorted(p_next):
-                            single_exp(p_next[n], n)
-
-                    for k in (0, 1, 2) if i == 3 else (i - 1,):
-                        left[k] = left_side(k, p_cube)
-                    for k in () if i == 3 else (6, 7, 8, 9) if i == 10 else (i - 4,):
-                        basis_function(k, left[k], q_cube, g, acc)
-
+        def store_result(r, acc):
             result = stage.tile([P, ROW_TILES, OUTPUTS], F32, name="result")
             for m in range(ROW_TILES):
                 nc.scalar.copy(out=result[:, m, :], in_=acc[m][:])
@@ -308,3 +273,84 @@ def tile_kanlayer_kernel(tc, x, knots, control_points, out):
                 out=out[r * ROWS : (r + 1) * ROWS, :].rearrange("(m p) o -> p m o", p=P),
                 in_=result[:],
             )
+
+        v_now = flip_rows(x_tiles)
+        vg = values(v_now, 0)
+        square = make_square(vg, 3)
+        single = {i: single_clamp(vg, i) for i in P_ONLY}
+        for i in P_ONLY:
+            single_log(vg, i, single[i])
+        single[11] = single_clamp(vg, 11)
+        cube = signed_cube(vg, 3, square)
+        sides = both_sides(cube, 3)
+        square = make_square(vg, 4)
+        for k in range(BASES):
+            prepare_weights(cp_sb, 0, k)
+        for i in P_ONLY:
+            single_exp(i, single[i])
+
+        acc = new_sums()
+        for r in range(ROUNDS):
+            for g in range(HALVES):
+                last = r == ROUNDS - 1 and g == HALVES - 1
+                vg = values(v_now, g)
+                if g == 0 and r < ROUNDS - 1:
+                    x_tiles = load_rows(r + 1)
+                p_cube = {i: single[i] for i in P_ONLY}
+                q_cube = {11: single[11]}
+                single = {}
+                left = {}
+
+                for i in BOTH:
+                    if i == 4:
+                        if g == HALVES - 1 and not last:
+                            v_now = flip_rows(x_tiles)
+                        v_after = None if last else values(v_now, (g + 1) % HALVES)
+                    p_cube[i], q_cube[i] = sides
+                    for ahead in (1, 2):
+                        n = i + ahead
+                        if n <= BOTH[-1]:
+                            source, knot = vg, n
+                        elif not last:
+                            source, knot = v_after, n - len(BOTH)
+                        else:
+                            continue
+                        if ahead == 1:
+                            sides = both_sides(signed_cube(source, knot, square), knot)
+                        else:
+                            square = make_square(source, knot)
+
+                    if i <= 5:
+                        single_log(vg, i + 8, q_cube[i + 8])
+                        if i < 5:
+                            q_cube[i + 9] = single_clamp(vg, i + 9)
+                    elif i <= 8 and not last:
+                        single_log(v_after, i - 6, single[i - 6])
+                    if i in (5, 6, 7) and not last:
+                        single[i - 5] = single_clamp(v_after, i - 5)
+                    if i == 9:
+                        single_exp(11, q_cube[11])
+                        single_exp(12, q_cube[12])
+                    if i == 10:
+                        single_exp(13, q_cube[13])
+                        for n in sorted(single):
+                            single_exp(n, single[n])
+
+                    if i == 3 and g == 0 and r > 0:
+                        store_result(r - 1, acc)
+                        acc = new_sums()
+
+                    for k in (0, 1, 2) if i == 3 else (i - 1,):
+                        left[k] = left_side(k, p_cube)
+                    for k in () if i == 3 else (6, 7, 8, 9) if i == 10 else (i - 4,):
+                        basis_function(k, left[k], q_cube, g, acc)
+
+                    if r == 0 and g == 0:
+                        if i == 3:
+                            cp_sb = load_points(1)
+                        elif 5 <= i <= 9:
+                            prepare_weights(cp_sb, 1, 2 * (i - 5))
+                            prepare_weights(cp_sb, 1, 2 * (i - 5) + 1)
+                if not last:
+                    single[11] = single_clamp(v_after, 11)
+        store_result(ROUNDS - 1, acc)

@@ -109,7 +109,7 @@ def tile_kanlayer_kernel(tc, x, knots, control_points, out):
         mx_pool = ctx.enter_context(tc.tile_pool(name="mx_pool", bufs=2))
         flip_psum = ctx.enter_context(tc.psum_pool(name="flip_psum", bufs=3))
         acc_psum = ctx.enter_context(tc.psum_pool(name="acc_psum", bufs=1))
-        ctx.enter_context(tc.manual_schedule(engines={mybir.EngineType.Activation}))
+        ctx.enter_context(tc.manual_schedule(engines={mybir.EngineType.Activation, mybir.EngineType.DVE}))
 
         def load_rows(r):
             tiles = []
@@ -149,18 +149,29 @@ def tile_kanlayer_kernel(tc, x, knots, control_points, out):
         w_codes = weights.tile([P, BASES, HALVES * OUTPUTS], U32, align_bytes=64)
         w_scales = weights.tile([P, BASES, HALVES * OUTPUTS], U8, align_bytes=64)
 
-        def prepare_weights(cp_sb, g, k):
+        def prepare_weights(cp_sb, k):
             w_flip = flip_psum.tile([P, PACK, P], BF16, name="flip")
             for t in range(PACK):
                 nc.tensor.transpose(w_flip[:, t, :], cp_sb[:, feature_columns(t), k], ident[:])
             w_grouped = stage.tile([P, OUTPUTS, PACK], BF16, name="w_grouped", align_bytes=64)
             nc.vector.tensor_copy(out=w_grouped[:], in_=w_flip[:].rearrange("p t o -> p o t"))
+            return w_grouped
+
+        def quantise_weights(w_grouped, g, k):
             o_cols = slice(g * OUTPUTS, (g + 1) * OUTPUTS)
             nc.vector.quantize_mx(
                 out=w_codes[:, k, o_cols].bitcast(FP8X4),
                 scales=w_scales[:, k, o_cols],
                 in_=w_grouped[:].rearrange("p o t -> p (o t)"),
             )
+
+        def prepare_all_weights(cp_sb, g, ks):
+            grouped = {}
+            for k in ks:
+                grouped[k] = prepare_weights(cp_sb, k)
+                if k - 1 in grouped:
+                    quantise_weights(grouped[k - 1], g, k - 1)
+            quantise_weights(grouped[ks[-1]], g, ks[-1])
 
         def single_clamp(vg, i):
             dist = single_pool.tile([P, CHUNK], F32, name="single%d" % i)
@@ -229,7 +240,7 @@ def tile_kanlayer_kernel(tc, x, knots, control_points, out):
             )
             return left
 
-        def basis_function(k, left, q_cube, g, acc):
+        def right_side(k, q_cube):
             right = stage.tile([P, CHUNK], BF16, name="right")
             nc.vector.scalar_tensor_tensor(
                 out=right[:],
@@ -239,8 +250,14 @@ def tile_kanlayer_kernel(tc, x, knots, control_points, out):
                 op0=ALU.mult,
                 op1=ALU.add,
             )
+            return right
+
+        def join_sides(left, right):
             basis = mx_pool.tile([P, CHUNK], BF16, name="basis", align_bytes=64)
             nc.vector.tensor_tensor(out=basis[:], in0=left[:], in1=right[:], op=ALU.max)
+            return basis
+
+        def multiply(basis, k, g, acc):
             b_codes = mx_pool.tile([P, ROWS], U32, name="b_codes", align_bytes=64)
             b_scales = mx_pool.tile([P, ROWS], U8, name="b_scales", align_bytes=64)
             nc.vector.quantize_mx(
@@ -284,12 +301,12 @@ def tile_kanlayer_kernel(tc, x, knots, control_points, out):
         cube = signed_cube(vg, 3, square)
         sides = both_sides(cube, 3)
         square = make_square(vg, 4)
-        for k in range(BASES):
-            prepare_weights(cp_sb, 0, k)
+        prepare_all_weights(cp_sb, 0, range(BASES))
         for i in P_ONLY:
             single_exp(i, single[i])
 
         acc = new_sums()
+        joined = []
         for r in range(ROUNDS):
             for g in range(HALVES):
                 last = r == ROUNDS - 1 and g == HALVES - 1
@@ -307,7 +324,7 @@ def tile_kanlayer_kernel(tc, x, knots, control_points, out):
                             v_now = flip_rows(x_tiles)
                         v_after = None if last else values(v_now, (g + 1) % HALVES)
                     p_cube[i], q_cube[i] = sides
-                    for ahead in (1, 2):
+                    for ahead in (2, 1):
                         n = i + ahead
                         if n <= BOTH[-1]:
                             source, knot = vg, n
@@ -318,7 +335,10 @@ def tile_kanlayer_kernel(tc, x, knots, control_points, out):
                         if ahead == 1:
                             sides = both_sides(signed_cube(source, knot, square), knot)
                         else:
-                            square = make_square(source, knot)
+                            square_after = make_square(source, knot)
+                    square = square_after
+                    if joined:
+                        multiply(*joined.pop())
 
                     if i <= 5:
                         single_log(vg, i + 8, q_cube[i + 8])
@@ -340,17 +360,23 @@ def tile_kanlayer_kernel(tc, x, knots, control_points, out):
                         store_result(r - 1, acc)
                         acc = new_sums()
 
+                    first = i - 4
+                    right = right_side(first, q_cube) if first >= 0 else None
                     for k in (0, 1, 2) if i == 3 else (i - 1,):
                         left[k] = left_side(k, p_cube)
-                    for k in () if i == 3 else (6, 7, 8, 9) if i == 10 else (i - 4,):
-                        basis_function(k, left[k], q_cube, g, acc)
+                    if first >= 0:
+                        joined.append((join_sides(left[first], right), first, g, acc))
+                    for k in (7, 8, 9) if i == 10 else ():
+                        right = right_side(k, q_cube)
+                        multiply(*joined.pop())
+                        joined.append((join_sides(left[k], right), k, g, acc))
 
                     if r == 0 and g == 0:
                         if i == 3:
                             cp_sb = load_points(1)
                         elif 5 <= i <= 9:
-                            prepare_weights(cp_sb, 1, 2 * (i - 5))
-                            prepare_weights(cp_sb, 1, 2 * (i - 5) + 1)
+                            prepare_all_weights(cp_sb, 1, range(2 * (i - 5), 2 * (i - 5) + 2))
                 if not last:
                     single[11] = single_clamp(v_after, 11)
+        multiply(*joined.pop())
         store_result(ROUNDS - 1, acc)

@@ -19,23 +19,24 @@ OUTPUTS = 128
 KNOTS = 14
 POINTS = 13
 BASES = 10
-HALVES = FEATURES // (P * PACK)
+PASS = P * PACK
+HALVES = FEATURES // PASS
 ROWS = 512
 ROW_TILES = ROWS // P
 ROUNDS = BATCH // ROWS
 CHUNK = ROWS * PACK
 TINY = 2.0**-60
 
-P_ONLY = (0, 1, 2)
-BOTH = (3, 4, 5, 6, 7, 8, 9, 10)
-Q_ONLY = (11, 12, 13)
+P_ONLY = (0, 1, 2, 3)
+BOTH = (4, 5, 6, 7, 8, 9)
+Q_ONLY = (10, 11, 12, 13)
 
 FLOPS = 2 * BATCH * BASES * FEATURES * OUTPUTS
 
 
 def feature_columns(n):
     g, t = divmod(n, PACK)
-    return slice(g * P * PACK + t, (g + 1) * P * PACK, PACK)
+    return slice(g * PASS + t, (g + 1) * PASS, PACK)
 
 
 def spline_constants(nc, pool, knots):
@@ -59,19 +60,17 @@ def spline_constants(nc, pool, knots):
     p_prod = pool.tile([P, cubes], F32)
     nc.vector.tensor_mul(out=p_prod[:], in0=d1[:, 0:cubes], in1=d2[:, 0:cubes])
     nc.vector.tensor_mul(out=p_prod[:], in0=p_prod[:], in1=d3[:, 0:cubes])
-    p_scale = pool.tile([P, cubes], F32)
-    nc.vector.reciprocal(out=p_scale[:], in_=p_prod[:])
+    p_factor = pool.tile([P, cubes], F32)
+    nc.vector.reciprocal(out=p_factor[:], in_=p_prod[:])
     q_prod = pool.tile([P, cubes], F32)
     nc.vector.tensor_mul(out=q_prod[:], in0=d1[:, 2 : 2 + cubes], in1=d2[:, 1 : 1 + cubes])
     nc.vector.tensor_mul(out=q_prod[:], in0=q_prod[:], in1=d3[:, 0:cubes])
-    q_recip = pool.tile([P, cubes], F32)
-    nc.vector.reciprocal(out=q_recip[:], in_=q_prod[:])
-    q_scale = pool.tile([P, cubes], F32)
-    nc.vector.tensor_scalar_mul(out=q_scale[:], in0=q_recip[:], scalar1=-1.0)
+    q_factor = pool.tile([P, cubes], F32)
+    nc.vector.reciprocal(out=q_factor[:], in_=q_prod[:])
     p_log = pool.tile([P, cubes], F32)
-    nc.scalar.activation(out=p_log[:], in_=p_scale[:], func=ACT.Ln)
+    nc.scalar.activation(out=p_log[:], in_=p_factor[:], func=ACT.Ln)
     q_log = pool.tile([P, cubes], F32)
-    nc.scalar.activation(out=q_log[:], in_=q_recip[:], func=ACT.Ln)
+    nc.scalar.activation(out=q_log[:], in_=q_factor[:], func=ACT.Ln)
 
     d1_recip = pool.tile([P, KNOTS - 1], F32)
     nc.vector.reciprocal(out=d1_recip[:], in_=d1[:])
@@ -81,16 +80,58 @@ def spline_constants(nc, pool, knots):
     nc.vector.tensor_mul(out=left_w[:], in0=neg_d4[:], in1=d1_recip[:, 0:BASES])
     right_w = pool.tile([P, BASES], F32)
     nc.vector.tensor_mul(out=right_w[:], in0=neg_d4[:], in1=d1_recip[:, 3 : 3 + BASES])
+
+    third_w = pool.tile([P, 2], F32)
+    third_den = pool.tile([P, 2], F32)
+    for n, (k, i, j, m) in enumerate(((0, 2, 0, 1), (9, 8, 11, 11))):
+        col = slice(n, n + 1)
+        nc.vector.tensor_mul(out=third_w[:, col], in0=d4[:, k : k + 1], in1=d3[:, i : i + 1])
+        nc.vector.tensor_mul(out=third_den[:, col], in0=d2[:, j : j + 1], in1=d1[:, m : m + 1])
+    third_recip = pool.tile([P, 2], F32)
+    nc.vector.reciprocal(out=third_recip[:], in_=third_den[:])
+    nc.vector.tensor_mul(out=third_w[:], in0=third_w[:], in1=third_recip[:])
+
+    neg_factor = pool.tile([P, 2], F32)
+    nc.vector.tensor_mul(out=neg_factor[:, 0:1], in0=q_factor[:, 1:2], in1=right_w[:, 1:2])
+    nc.vector.tensor_mul(out=neg_factor[:, 1:2], in0=p_factor[:, 9:10], in1=left_w[:, 8:9])
+    factor = pool.tile([P, 2], F32)
+    nc.vector.tensor_scalar_mul(out=factor[:], in0=neg_factor[:], scalar1=-1.0)
+    half = pool.tile([P, 2], F32)
+    nc.gpsimd.memset(half[:], 0.5)
+    root = pool.tile([P, 2], F32)
+    nc.gpsimd.tensor_tensor(out=root[:], in0=factor[:], in1=half[:], op=ALU.pow)
+    root_bias = pool.tile([P, 2], F32)
+    nc.vector.tensor_mul(out=root_bias[:, 0:1], in0=root[:, 0:1], in1=neg_t[:, 4:5])
+    nc.vector.tensor_mul(out=root_bias[:, 1:2], in0=root[:, 1:2], in1=neg_t[:, 9:10])
+    neg_recip = pool.tile([P, 2], F32)
+    nc.vector.reciprocal(out=neg_recip[:], in_=neg_factor[:])
+
+    p_side = pool.tile([P, 6], F32)
+    q_side = pool.tile([P, 6], F32)
+    nc.vector.tensor_copy(out=p_side[:, 0:5], in_=p_factor[:, 4:9])
+    nc.vector.tensor_scalar_mul(out=q_side[:], in0=q_factor[:, 1:7], scalar1=-1.0)
+    recip = pool.tile([P, 1], F32)
+    nc.vector.tensor_scalar_mul(out=recip[:], in0=neg_recip[:, 0:1], scalar1=-1.0)
+    nc.vector.tensor_mul(out=p_side[:, 0:1], in0=p_factor[:, 4:5], in1=recip[:])
+    nc.vector.tensor_mul(out=q_side[:, 0:1], in0=q_side[:, 0:1], in1=recip[:])
+    nc.vector.tensor_mul(out=p_side[:, 5:6], in0=p_factor[:, 9:10], in1=neg_recip[:, 1:2])
+    nc.vector.tensor_mul(out=q_side[:, 5:6], in0=q_side[:, 5:6], in1=neg_recip[:, 1:2])
+    tiny = pool.tile([P, 1], F32)
+    nc.vector.memset(tiny[:], TINY)
     return {
         "t": t,
         "neg_t": neg_t,
         "first_bias": first_bias,
-        "p_scale": p_scale,
-        "q_scale": q_scale,
+        "tiny": tiny,
         "p_log": p_log,
         "q_log": q_log,
         "left_w": left_w,
         "right_w": right_w,
+        "third_w": third_w,
+        "root": root,
+        "root_bias": root_bias,
+        "p_side": p_side,
+        "q_side": q_side,
     }
 
 
@@ -99,17 +140,22 @@ def tile_kanlayer_kernel(tc, x, knots, control_points, out):
     with ExitStack() as ctx:
         consts = ctx.enter_context(tc.tile_pool(name="consts", bufs=1))
         weights = ctx.enter_context(tc.tile_pool(name="weights", bufs=1))
-        x_pool = ctx.enter_context(tc.tile_pool(name="x_pool", bufs=ROW_TILES))
-        v_pool = ctx.enter_context(tc.tile_pool(name="v_pool", bufs=2))
+        x_pool = ctx.enter_context(tc.tile_pool(name="x_pool", bufs=3))
+        v_pool = ctx.enter_context(tc.tile_pool(name="v_pool", bufs=3))
         stage = ctx.enter_context(tc.tile_pool(name="stage", bufs=2))
+        result_pool = ctx.enter_context(tc.tile_pool(name="result_pool", bufs=1))
         single_pool = ctx.enter_context(tc.tile_pool(name="single_pool", bufs=1))
-        cube_pool = ctx.enter_context(tc.tile_pool(name="cube_pool", bufs=2))
+        square_pool = ctx.enter_context(tc.tile_pool(name="square_pool", bufs=2))
+        cube_pool = ctx.enter_context(tc.tile_pool(name="cube_pool", bufs=3))
         side_pool = ctx.enter_context(tc.tile_pool(name="side_pool", bufs=3))
-        left_pool = ctx.enter_context(tc.tile_pool(name="left_pool", bufs=6))
+        edge_pool = ctx.enter_context(tc.tile_pool(name="edge_pool", bufs=1))
+        left_pool = ctx.enter_context(tc.tile_pool(name="left_pool", bufs=5))
         mx_pool = ctx.enter_context(tc.tile_pool(name="mx_pool", bufs=2))
         flip_psum = ctx.enter_context(tc.psum_pool(name="flip_psum", bufs=3))
         acc_psum = ctx.enter_context(tc.psum_pool(name="acc_psum", bufs=1))
-        ctx.enter_context(tc.manual_schedule(engines={mybir.EngineType.Activation, mybir.EngineType.DVE}))
+        ctx.enter_context(
+            tc.manual_schedule(engines={mybir.EngineType.Activation, mybir.EngineType.DVE})
+        )
 
         def load_rows(r):
             tiles = []
@@ -120,90 +166,99 @@ def tile_kanlayer_kernel(tc, x, knots, control_points, out):
                 tiles.append(x_sb)
             return tiles
 
+        def flip_tile(x_sb, m, v, copy):
+            x_flip = flip_psum.tile([P, HALVES * PACK, P], BF16, name="flip")
+            for n in range(HALVES * PACK):
+                nc.tensor.transpose(x_flip[:, n, :], x_sb[:, feature_columns(n)], ident[:])
+            for g in range(HALVES):
+                copy(
+                    out=v[g][:, m * P : (m + 1) * P, :],
+                    in_=x_flip[:, g * PACK : (g + 1) * PACK, :].rearrange("p t b -> p b t"),
+                )
+
+        def new_values():
+            return [v_pool.tile([P, ROWS, PACK], BF16, name="v") for g in range(HALVES)]
+
+        def flat(v):
+            return v[:].rearrange("p b t -> p (b t)")
+
+        w_codes = weights.tile([P, HALVES, BASES, OUTPUTS], U32, align_bytes=64)
+        w_scales = weights.tile([P, HALVES, BASES, OUTPUTS], U8, align_bytes=64)
+
         def load_points(g):
-            cp_sb = weights.tile([P, P * PACK, POINTS], BF16, name="cp_sb")
-            first = g * P * PACK
-            nc.sync.dma_start(out=cp_sb[:], in_=control_points[:, first : first + P * PACK, :])
+            cp_sb = single_pool.tile([P, PASS, POINTS], BF16, name="last%d" % g)
+            nc.sync.dma_start(
+                out=cp_sb[:], in_=control_points[:, g * PASS : (g + 1) * PASS, :]
+            )
             return cp_sb
 
-        x_tiles = load_rows(0)
-        c = spline_constants(nc, consts, knots)
-        cp_sb = load_points(0)
-        ident = consts.tile([P, P], BF16)
-        make_identity(nc, ident[:])
-
-        def flip_rows(x_tiles):
-            v = v_pool.tile([P, HALVES, ROWS, PACK], BF16, name="v")
-            for m in range(ROW_TILES):
-                x_flip = flip_psum.tile([P, HALVES * PACK, P], BF16, name="flip")
-                for n in range(HALVES * PACK):
+        def flip_weights(cp_sb, k):
+            w_flip = flip_psum.tile([P, 2, PACK, P], BF16, name="flip")
+            for n in range(2):
+                for t in range(PACK):
                     nc.tensor.transpose(
-                        x_flip[:, n, :], x_tiles[m][:, feature_columns(n)], ident[:]
+                        w_flip[:, n, t, :], cp_sb[:, feature_columns(t), k + n], ident[:]
                     )
-                nc.scalar.copy(
-                    out=v[:, :, m * P : (m + 1) * P, :],
-                    in_=x_flip[:].rearrange("p (g t) b -> p g b t", g=HALVES),
-                )
-            return v
-
-        w_codes = weights.tile([P, BASES, HALVES * OUTPUTS], U32, align_bytes=64)
-        w_scales = weights.tile([P, BASES, HALVES * OUTPUTS], U8, align_bytes=64)
-
-        def prepare_weights(cp_sb, k):
-            w_flip = flip_psum.tile([P, PACK, P], BF16, name="flip")
-            for t in range(PACK):
-                nc.tensor.transpose(w_flip[:, t, :], cp_sb[:, feature_columns(t), k], ident[:])
-            w_grouped = stage.tile([P, OUTPUTS, PACK], BF16, name="w_grouped", align_bytes=64)
-            nc.vector.tensor_copy(out=w_grouped[:], in_=w_flip[:].rearrange("p t o -> p o t"))
+            w_grouped = stage.tile([P, 2, OUTPUTS, PACK], BF16, name="w_grouped", align_bytes=64)
+            nc.vector.tensor_copy(out=w_grouped[:], in_=w_flip[:].rearrange("p n t o -> p n o t"))
             return w_grouped
 
         def quantise_weights(w_grouped, g, k):
-            o_cols = slice(g * OUTPUTS, (g + 1) * OUTPUTS)
             nc.vector.quantize_mx(
-                out=w_codes[:, k, o_cols].bitcast(FP8X4),
-                scales=w_scales[:, k, o_cols],
-                in_=w_grouped[:].rearrange("p o t -> p (o t)"),
+                out=w_codes[:, g, k : k + 2, :].rearrange("p n o -> p (n o)").bitcast(FP8X4),
+                scales=w_scales[:, g, k : k + 2, :].rearrange("p n o -> p (n o)"),
+                in_=w_grouped[:].rearrange("p n o t -> p (n o t)"),
             )
 
-        def prepare_all_weights(cp_sb, g, ks):
-            grouped = {}
-            for k in ks:
-                grouped[k] = prepare_weights(cp_sb, k)
-                if k - 1 in grouped:
-                    quantise_weights(grouped[k - 1], g, k - 1)
-            quantise_weights(grouped[ks[-1]], g, ks[-1])
+        def clamp_distance(dist, vg, i):
+            on_right = i in P_ONLY
+            nc.vector.tensor_scalar(
+                out=dist,
+                in0=vg,
+                scalar1=c["t"][:, i : i + 1],
+                scalar2=TINY if on_right else -TINY,
+                op0=ALU.subtract,
+                op1=ALU.max if on_right else ALU.min,
+            )
 
-        def single_clamp(vg, i):
-            dist = single_pool.tile([P, CHUNK], F32, name="single%d" % i)
-            if i > 0:
-                on_right = i in P_ONLY
-                nc.vector.tensor_scalar(
-                    out=dist[:],
-                    in0=vg,
-                    scalar1=c["t"][:, i : i + 1],
-                    scalar2=TINY if on_right else -TINY,
-                    op0=ALU.subtract,
-                    op1=ALU.max if on_right else ALU.min,
-                )
-            return dist
-
-        def single_log(vg, i, dist):
+        def log_distance(dist, vg, i, clamp=False):
             if i == 0:
-                nc.scalar.activation(out=dist[:], in_=vg, func=ACT.Ln, bias=c["first_bias"][:])
+                nc.scalar.activation(out=dist, in_=vg, func=ACT.Ln, bias=c["first_bias"][:])
+            elif clamp:
+                nc.scalar.activation(
+                    out=dist, in_=vg, func=ACT.Relu, scale=-1.0, bias=c["t"][:, i : i + 1]
+                )
+                nc.scalar.activation(out=dist, in_=dist, func=ACT.Ln, bias=c["tiny"][:])
             else:
                 sign = 1.0 if i in P_ONLY else -1.0
-                nc.scalar.activation(out=dist[:], in_=dist[:], func=ACT.Ln, scale=sign)
+                nc.scalar.activation(out=dist, in_=dist, func=ACT.Ln, scale=sign)
 
-        def single_exp(i, log):
+        def cube_distance(dist, i):
             factor = c["p_log"][:, i : i + 1] if i in P_ONLY else c["q_log"][:, i - 3 : i - 2]
-            nc.scalar.activation(out=log[:], in_=log[:], func=ACT.Exp, scale=3.0, bias=factor)
+            nc.scalar.activation(out=dist, in_=dist, func=ACT.Exp, scale=3.0, bias=factor)
+
+        def new_first(i):
+            tile = single_pool.tile([P, CHUNK], F32, name="first%d" % i)
+            return tile[:]
+
+        def new_last():
+            pairs = [single_pool.tile([P, 2, CHUNK], F32, name="last%d" % n) for n in range(2)]
+            return {i: pairs[(i - 10) // 2][:, i % 2, :] for i in Q_ONLY}
 
         def make_square(vg, i):
-            square = cube_pool.tile([P, CHUNK], F32, name="square")
-            nc.scalar.activation(
-                out=square[:], in_=vg, func=ACT.Square, bias=c["neg_t"][:, i : i + 1]
-            )
+            square = square_pool.tile([P, CHUNK], F32, name="square")
+            if i in (4, 9):
+                col = slice(0, 1) if i == 4 else slice(1, 2)
+                bias, scale = c["root_bias"][:, col], c["root"][:, col]
+            else:
+                bias, scale = c["neg_t"][:, i : i + 1], 1.0
+            nc.scalar.activation(out=square[:], in_=vg, func=ACT.Square, bias=bias, scale=scale)
             return square
+
+        def negate(vg):
+            negated = stage.tile([P, CHUNK], BF16, name="right")
+            nc.vector.tensor_scalar_mul(out=negated[:], in0=vg, scalar1=-1.0)
+            return negated[:]
 
         def signed_cube(vg, i, square):
             cube = cube_pool.tile([P, CHUNK], F32, name="cube")
@@ -212,49 +267,63 @@ def tile_kanlayer_kernel(tc, x, knots, control_points, out):
                 in0=vg,
                 scalar=c["t"][:, i : i + 1],
                 in1=square[:],
-                op0=ALU.subtract,
+                op0=ALU.add if i == 9 else ALU.subtract,
                 op1=ALU.mult,
             )
             return cube
 
-        def both_sides(cube, i):
-            p_cube = side_pool.tile([P, CHUNK], F32, name="p_cube")
-            nc.scalar.activation(
-                out=p_cube[:], in_=cube[:], func=ACT.Relu, scale=c["p_scale"][:, i : i + 1]
-            )
-            q_cube = side_pool.tile([P, CHUNK], F32, name="q_cube")
-            nc.scalar.activation(
-                out=q_cube[:], in_=cube[:], func=ACT.Relu, scale=c["q_scale"][:, i - 3 : i - 2]
-            )
-            return p_cube, q_cube
+        def relu_of(cube, scale, tile):
+            nc.scalar.activation(out=tile[:], in_=cube[:], func=ACT.Relu, scale=scale)
+            return tile[:]
 
-        def left_side(k, p_cube):
+        def make_sides(cube, i):
+            p_tile = (
+                edge_pool.tile([P, CHUNK], BF16, name="last_edge")
+                if i == 9
+                else side_pool.tile([P, CHUNK], F32, name="p_cube")
+            )
+            p_side = relu_of(cube, c["p_side"][:, i - 4 : i - 3], p_tile)
+            q_tile = (
+                edge_pool.tile([P, CHUNK], BF16, name="first_edge")
+                if i == 4
+                else side_pool.tile([P, CHUNK], F32, name="q_cube")
+            )
+            q_side = relu_of(cube, c["q_side"][:, i - 4 : i - 3], q_tile)
+            return p_side, q_side
+
+        def combine(out, in0, factor, in1):
+            nc.vector.scalar_tensor_tensor(
+                out=out, in0=in0, scalar=factor, in1=in1, op0=ALU.mult, op1=ALU.add
+            )
+            return out
+
+        def add_negative(out, cube, in1):
+            nc.vector.scalar_tensor_tensor(
+                out=out, in0=cube[:], scalar=0.0, in1=in1, op0=ALU.min, op1=ALU.add
+            )
+            return out
+
+        def new_left():
             left = left_pool.tile([P, CHUNK], BF16, name="left")
-            nc.vector.scalar_tensor_tensor(
-                out=left[:],
-                in0=p_cube[k + 1][:],
-                scalar=c["left_w"][:, k : k + 1],
-                in1=p_cube[k][:],
-                op0=ALU.mult,
-                op1=ALU.add,
-            )
-            return left
+            return left[:]
 
-        def right_side(k, q_cube):
+        def new_right():
             right = stage.tile([P, CHUNK], BF16, name="right")
-            nc.vector.scalar_tensor_tensor(
-                out=right[:],
-                in0=q_cube[k + 3][:],
-                scalar=c["right_w"][:, k : k + 1],
-                in1=q_cube[k + 4][:],
-                op0=ALU.mult,
-                op1=ALU.add,
-            )
-            return right
+            return right[:]
 
-        def join_sides(left, right):
+        def left_side(k, p_cube, cube):
+            if k == 8:
+                return add_negative(new_left(), cube[9], p_cube[8])
+            return combine(new_left(), p_cube[k + 1], c["left_w"][:, k : k + 1], p_cube[k])
+
+        def right_side(k, q_cube, cube):
+            if k == 1:
+                return add_negative(new_right(), cube[4], q_cube[5])
+            return combine(new_right(), q_cube[k + 3], c["right_w"][:, k : k + 1], q_cube[k + 4])
+
+        def join(one, other, op):
             basis = mx_pool.tile([P, CHUNK], BF16, name="basis", align_bytes=64)
-            nc.vector.tensor_tensor(out=basis[:], in0=left[:], in1=right[:], op=ALU.max)
+            nc.vector.tensor_tensor(out=basis[:], in0=one, in1=other, op=op)
             return basis
 
         def multiply(basis, k, g, acc):
@@ -263,27 +332,23 @@ def tile_kanlayer_kernel(tc, x, knots, control_points, out):
             nc.vector.quantize_mx(
                 out=b_codes[:].bitcast(FP8X4), scales=b_scales[:], in_=basis[:]
             )
-            o_cols = slice(g * OUTPUTS, (g + 1) * OUTPUTS)
             for m in range(ROW_TILES):
                 b_cols = slice(m * P, (m + 1) * P)
                 nc.tensor.matmul_mx(
                     out=acc[m][:],
                     lhsT=b_codes[:, b_cols].bitcast(FP8X4),
                     lhsT_scale=b_scales[:, b_cols],
-                    rhs=w_codes[:, k, o_cols].bitcast(FP8X4),
-                    rhs_scale=w_scales[:, k, o_cols],
+                    rhs=w_codes[:, g, k, :].bitcast(FP8X4),
+                    rhs_scale=w_scales[:, g, k, :],
                     start=(g == 0 and k == 0),
                     stop=(g == HALVES - 1 and k == BASES - 1),
                 )
-
-        def values(v, g):
-            return v[:, g, :, :].rearrange("p b t -> p (b t)")
 
         def new_sums():
             return [acc_psum.tile([P, OUTPUTS], F32, name="acc%d" % m) for m in range(ROW_TILES)]
 
         def store_result(r, acc):
-            result = stage.tile([P, ROW_TILES, OUTPUTS], F32, name="result")
+            result = result_pool.tile([P, ROW_TILES, OUTPUTS], F32, name="result")
             for m in range(ROW_TILES):
                 nc.scalar.copy(out=result[:, m, :], in_=acc[m][:])
             nc.sync.dma_start(
@@ -291,92 +356,127 @@ def tile_kanlayer_kernel(tc, x, knots, control_points, out):
                 in_=result[:],
             )
 
-        v_now = flip_rows(x_tiles)
-        vg = values(v_now, 0)
-        square = make_square(vg, 3)
-        single = {i: single_clamp(vg, i) for i in P_ONLY}
-        for i in P_ONLY:
-            single_log(vg, i, single[i])
-        single[11] = single_clamp(vg, 11)
-        cube = signed_cube(vg, 3, square)
-        sides = both_sides(cube, 3)
+        c = spline_constants(nc, consts, knots)
+        x_tiles = load_rows(0)
+        cp_tiles = [load_points(g) for g in range(HALVES)]
+        ident = consts.tile([P, P], BF16)
+        make_identity(nc, ident[:])
+
+        v_now = new_values()
+        for m in range(ROW_TILES):
+            flip_tile(x_tiles[m], m, v_now, nc.vector.tensor_copy if m % 2 else nc.scalar.copy)
+        vg = flat(v_now[0])
+        cube_next = {}
         square = make_square(vg, 4)
-        prepare_all_weights(cp_sb, 0, range(BASES))
+        square_after = make_square(vg, 5)
+        first = {i: new_first(i) for i in P_ONLY}
+        for i in P_ONLY[1:]:
+            clamp_distance(first[i], vg, i)
         for i in P_ONLY:
-            single_exp(i, single[i])
+            log_distance(first[i], vg, i)
+        for i in P_ONLY:
+            cube_distance(first[i], i)
+        cube_next[4] = signed_cube(vg, 4, square)
+        sides = make_sides(cube_next[4], 4)
+        square = square_after
+        grouped = None
+        for g in range(HALVES):
+            for k in range(0, BASES, 2):
+                w_grouped = flip_weights(cp_tiles[g], k)
+                if grouped:
+                    quantise_weights(*grouped)
+                grouped = (w_grouped, g, k)
+        quantise_weights(*grouped)
+        negated = None
 
         acc = new_sums()
-        joined = []
+        waiting = []
         for r in range(ROUNDS):
             for g in range(HALVES):
-                last = r == ROUNDS - 1 and g == HALVES - 1
-                vg = values(v_now, g)
-                if g == 0 and r < ROUNDS - 1:
-                    x_tiles = load_rows(r + 1)
-                p_cube = {i: single[i] for i in P_ONLY}
-                q_cube = {11: single[11]}
-                single = {}
+                final = r == ROUNDS - 1 and g == HALVES - 1
+                vg = flat(v_now[g])
+                p_cube = dict(first)
+                q_cube = new_last()
+                cube = dict(cube_next)
                 left = {}
 
                 for i in BOTH:
+                    if i == 4 and g == HALVES - 1 and not final:
+                        v_now = new_values()
+                        for m in range(ROW_TILES):
+                            flip_tile(x_tiles[m], m, v_now, nc.scalar.copy)
                     if i == 4:
-                        if g == HALVES - 1 and not last:
-                            v_now = flip_rows(x_tiles)
-                        v_after = None if last else values(v_now, (g + 1) % HALVES)
+                        v_after = None if final else flat(v_now[(g + 1) % HALVES])
                     p_cube[i], q_cube[i] = sides
-                    for ahead in (2, 1):
-                        n = i + ahead
-                        if n <= BOTH[-1]:
-                            source, knot = vg, n
-                        elif not last:
-                            source, knot = v_after, n - len(BOTH)
-                        else:
-                            continue
-                        if ahead == 1:
-                            sides = both_sides(signed_cube(source, knot, square), knot)
-                        else:
-                            square_after = make_square(source, knot)
+                    if i + 2 <= BOTH[-1]:
+                        square_after = make_square(vg, i + 2)
+                    elif not final:
+                        square_after = make_square(v_after, i + 2 - len(BOTH))
+                    if i < BOTH[-1]:
+                        source = negated if i + 1 == 9 else vg
+                        cube[i + 1] = signed_cube(source, i + 1, square)
+                        sides = make_sides(cube[i + 1], i + 1)
+                    elif not final:
+                        cube_next = {4: signed_cube(v_after, 4, square)}
+                        sides = make_sides(cube_next[4], 4)
                     square = square_after
-                    if joined:
-                        multiply(*joined.pop())
+                    if waiting:
+                        multiply(*waiting.pop())
 
-                    if i <= 5:
-                        single_log(vg, i + 8, q_cube[i + 8])
-                        if i < 5:
-                            q_cube[i + 9] = single_clamp(vg, i + 9)
-                    elif i <= 8 and not last:
-                        single_log(v_after, i - 6, single[i - 6])
-                    if i in (5, 6, 7) and not last:
-                        single[i - 5] = single_clamp(v_after, i - 5)
+                    by_scalar = Q_ONLY if final else (13,)
+                    late = (12, 13) if final else (13,) if g == HALVES - 1 else ()
+                    for n in Q_ONLY:
+                        if i == (5 if n in late else 4):
+                            if n not in by_scalar:
+                                clamp_distance(q_cube[n], vg, n)
+                            log_distance(q_cube[n], vg, n, clamp=n in by_scalar)
+                    if not final:
+                        if i == 5:
+                            first = {n: new_first(n) for n in P_ONLY}
+                        if 5 <= i <= 8:
+                            log_distance(first[i - 5], v_after, i - 5)
+                        if 5 <= i <= 7:
+                            clamp_distance(first[i - 4], v_after, i - 4)
+                    if i == 8:
+                        cube_distance(q_cube[10], 10)
                     if i == 9:
-                        single_exp(11, q_cube[11])
-                        single_exp(12, q_cube[12])
-                    if i == 10:
-                        single_exp(13, q_cube[13])
-                        for n in sorted(single):
-                            single_exp(n, single[n])
+                        cube_distance(q_cube[11], 11)
+                        cube_distance(q_cube[12], 12)
+                        cube_distance(q_cube[13], 13)
+                        if not final:
+                            for n in P_ONLY:
+                                cube_distance(first[n], n)
 
-                    if i == 3 and g == 0 and r > 0:
+                    if i == 4 and g == 0 and r > 0:
                         store_result(r - 1, acc)
                         acc = new_sums()
+                    if i == 5 and g == 0 and r < ROUNDS - 1:
+                        x_tiles = load_rows(r + 1)
 
-                    first = i - 4
-                    right = right_side(first, q_cube) if first >= 0 else None
-                    for k in (0, 1, 2) if i == 3 else (i - 1,):
-                        left[k] = left_side(k, p_cube)
-                    if first >= 0:
-                        joined.append((join_sides(left[first], right), first, g, acc))
-                    for k in (7, 8, 9) if i == 10 else ():
-                        right = right_side(k, q_cube)
-                        multiply(*joined.pop())
-                        joined.append((join_sides(left[k], right), k, g, acc))
+                    if i == 4:
+                        two = combine(p_cube[0], p_cube[1], c["left_w"][:, 0:1], p_cube[0])
+                        left[1] = left_side(1, p_cube, cube)
+                        three = combine(new_right(), p_cube[2], c["third_w"][:, 0:1], two)
+                        left[2] = left_side(2, p_cube, cube)
+                        left[3] = left_side(3, p_cube, cube)
+                        waiting.append((join(three, q_cube[4], ALU.min), 0, g, acc))
+                    else:
+                        k = i - 4
+                        right = right_side(k, q_cube, cube)
+                        left[i - 1] = left_side(i - 1, p_cube, cube)
+                        if i == 7:
+                            negated = negate(vg)
+                        waiting.append((join(left[k], right, ALU.max), k, g, acc))
 
-                    if r == 0 and g == 0:
-                        if i == 3:
-                            cp_sb = load_points(1)
-                        elif 5 <= i <= 9:
-                            prepare_all_weights(cp_sb, 1, range(2 * (i - 5), 2 * (i - 5) + 2))
-                if not last:
-                    single[11] = single_clamp(v_after, 11)
-        multiply(*joined.pop())
+                for k in (6, 7, 8):
+                    right = right_side(k, q_cube, cube)
+                    multiply(*waiting.pop())
+                    waiting.append((join(left[k], right, ALU.max), k, g, acc))
+                    if k == 7:
+                        two = combine(q_cube[13], q_cube[12], c["right_w"][:, 9:10], q_cube[13])
+                three = combine(new_right(), q_cube[11], c["third_w"][:, 1:2], two)
+                multiply(*waiting.pop())
+                waiting.append((join(three, p_cube[9], ALU.min), 9, g, acc))
+
+        multiply(*waiting.pop())
         store_result(ROUNDS - 1, acc)

@@ -25,6 +25,7 @@ ROWS = 512
 ROW_TILES = ROWS // P
 ROUNDS = BATCH // ROWS
 CHUNK = ROWS * PACK
+BOUND = 2.0**100
 TINY = 2.0**-60
 
 P_ONLY = (0, 1, 2, 3)
@@ -91,31 +92,28 @@ def spline_constants(nc, pool, knots):
     nc.vector.reciprocal(out=third_recip[:], in_=third_den[:])
     nc.vector.tensor_mul(out=third_w[:], in0=third_w[:], in1=third_recip[:])
 
-    neg_factor = pool.tile([P, 2], F32)
-    nc.vector.tensor_mul(out=neg_factor[:, 0:1], in0=q_factor[:, 1:2], in1=right_w[:, 1:2])
-    nc.vector.tensor_mul(out=neg_factor[:, 1:2], in0=p_factor[:, 9:10], in1=left_w[:, 8:9])
-    factor = pool.tile([P, 2], F32)
-    nc.vector.tensor_scalar_mul(out=factor[:], in0=neg_factor[:], scalar1=-1.0)
-    half = pool.tile([P, 2], F32)
+    both = len(BOTH)
+    factor = pool.tile([P, both], F32)
+    nc.vector.tensor_copy(out=factor[:], in_=p_factor[:, 4 : 4 + both])
+    nc.vector.tensor_mul(out=factor[:, 0:1], in0=q_factor[:, 1:2], in1=right_w[:, 1:2])
+    nc.vector.tensor_scalar_mul(out=factor[:, 0:1], in0=factor[:, 0:1], scalar1=-1.0)
+    nc.vector.tensor_mul(out=factor[:, 5:6], in0=p_factor[:, 9:10], in1=left_w[:, 8:9])
+    nc.vector.tensor_scalar_mul(out=factor[:, 5:6], in0=factor[:, 5:6], scalar1=-1.0)
+    half = pool.tile([P, both], F32)
     nc.gpsimd.memset(half[:], 0.5)
-    root = pool.tile([P, 2], F32)
+    root = pool.tile([P, both], F32)
     nc.gpsimd.tensor_tensor(out=root[:], in0=factor[:], in1=half[:], op=ALU.pow)
-    root_bias = pool.tile([P, 2], F32)
-    nc.vector.tensor_mul(out=root_bias[:, 0:1], in0=root[:, 0:1], in1=neg_t[:, 4:5])
-    nc.vector.tensor_mul(out=root_bias[:, 1:2], in0=root[:, 1:2], in1=neg_t[:, 9:10])
-    neg_recip = pool.tile([P, 2], F32)
-    nc.vector.reciprocal(out=neg_recip[:], in_=neg_factor[:])
+    root_bias = pool.tile([P, both], F32)
+    nc.vector.tensor_mul(out=root_bias[:], in0=root[:], in1=neg_t[:, 4 : 4 + both])
+    recip = pool.tile([P, both], F32)
+    nc.vector.reciprocal(out=recip[:], in_=factor[:])
+    nc.vector.tensor_scalar_mul(out=recip[:, 5:6], in0=recip[:, 5:6], scalar1=-1.0)
 
-    p_side = pool.tile([P, 6], F32)
-    q_side = pool.tile([P, 6], F32)
-    nc.vector.tensor_copy(out=p_side[:, 0:5], in_=p_factor[:, 4:9])
-    nc.vector.tensor_scalar_mul(out=q_side[:], in0=q_factor[:, 1:7], scalar1=-1.0)
-    recip = pool.tile([P, 1], F32)
-    nc.vector.tensor_scalar_mul(out=recip[:], in0=neg_recip[:, 0:1], scalar1=-1.0)
-    nc.vector.tensor_mul(out=p_side[:, 0:1], in0=p_factor[:, 4:5], in1=recip[:])
-    nc.vector.tensor_mul(out=q_side[:, 0:1], in0=q_side[:, 0:1], in1=recip[:])
-    nc.vector.tensor_mul(out=p_side[:, 5:6], in0=p_factor[:, 9:10], in1=neg_recip[:, 1:2])
-    nc.vector.tensor_mul(out=q_side[:, 5:6], in0=q_side[:, 5:6], in1=neg_recip[:, 1:2])
+    p_side = pool.tile([P, both], F32)
+    nc.vector.tensor_mul(out=p_side[:], in0=p_factor[:, 4 : 4 + both], in1=recip[:])
+    q_side = pool.tile([P, both], F32)
+    nc.vector.tensor_scalar_mul(out=q_side[:], in0=q_factor[:, 1 : 1 + both], scalar1=-1.0)
+    nc.vector.tensor_mul(out=q_side[:], in0=q_side[:], in1=recip[:])
     tiny = pool.tile([P, 1], F32)
     nc.vector.memset(tiny[:], TINY)
     return {
@@ -140,18 +138,19 @@ def tile_kanlayer_kernel(tc, x, knots, control_points, out):
     with ExitStack() as ctx:
         consts = ctx.enter_context(tc.tile_pool(name="consts", bufs=1))
         weights = ctx.enter_context(tc.tile_pool(name="weights", bufs=1))
-        x_pool = ctx.enter_context(tc.tile_pool(name="x_pool", bufs=3))
-        v_pool = ctx.enter_context(tc.tile_pool(name="v_pool", bufs=3))
+        x_pool = ctx.enter_context(tc.tile_pool(name="x_pool", bufs=ROW_TILES))
+        v_pool = ctx.enter_context(tc.tile_pool(name="v_pool", bufs=2))
         stage = ctx.enter_context(tc.tile_pool(name="stage", bufs=2))
         result_pool = ctx.enter_context(tc.tile_pool(name="result_pool", bufs=1))
         single_pool = ctx.enter_context(tc.tile_pool(name="single_pool", bufs=1))
         square_pool = ctx.enter_context(tc.tile_pool(name="square_pool", bufs=2))
         cube_pool = ctx.enter_context(tc.tile_pool(name="cube_pool", bufs=3))
-        side_pool = ctx.enter_context(tc.tile_pool(name="side_pool", bufs=3))
+        p_pool = ctx.enter_context(tc.tile_pool(name="p_pool", bufs=2))
+        q_pool = ctx.enter_context(tc.tile_pool(name="q_pool", bufs=3))
         edge_pool = ctx.enter_context(tc.tile_pool(name="edge_pool", bufs=1))
         left_pool = ctx.enter_context(tc.tile_pool(name="left_pool", bufs=5))
         mx_pool = ctx.enter_context(tc.tile_pool(name="mx_pool", bufs=2))
-        flip_psum = ctx.enter_context(tc.psum_pool(name="flip_psum", bufs=3))
+        flip_psum = ctx.enter_context(tc.psum_pool(name="flip_psum", bufs=4))
         acc_psum = ctx.enter_context(tc.psum_pool(name="acc_psum", bufs=1))
         ctx.enter_context(
             tc.manual_schedule(engines={mybir.EngineType.Activation, mybir.EngineType.DVE})
@@ -166,21 +165,22 @@ def tile_kanlayer_kernel(tc, x, knots, control_points, out):
                 tiles.append(x_sb)
             return tiles
 
-        def flip_tile(x_sb, m, v, copy):
-            x_flip = flip_psum.tile([P, HALVES * PACK, P], BF16, name="flip")
-            for n in range(HALVES * PACK):
-                nc.tensor.transpose(x_flip[:, n, :], x_sb[:, feature_columns(n)], ident[:])
-            for g in range(HALVES):
-                copy(
-                    out=v[g][:, m * P : (m + 1) * P, :],
-                    in_=x_flip[:, g * PACK : (g + 1) * PACK, :].rearrange("p t b -> p b t"),
-                )
-
-        def new_values():
-            return [v_pool.tile([P, ROWS, PACK], BF16, name="v") for g in range(HALVES)]
-
-        def flat(v):
-            return v[:].rearrange("p b t -> p (b t)")
+        def flip_values(x_tiles, g, copies):
+            v = v_pool.tile([P, ROWS, PACK], BF16, name="v")
+            banks = []
+            for pair, copy in enumerate(copies):
+                bank = flip_psum.tile([P, PACK, 2 * P], BF16, name="flip")
+                for n in range(2):
+                    for t in range(PACK):
+                        nc.tensor.transpose(
+                            bank[:, t, n * P : (n + 1) * P],
+                            x_tiles[2 * pair + n][:, feature_columns(g * PACK + t)],
+                            ident[:],
+                        )
+                view = bank[:].rearrange("p t b -> p b t")
+                copy(out=v[:, 2 * pair * P : 2 * (pair + 1) * P, :], in_=view)
+                banks.append(view)
+            return v[:].rearrange("p b t -> p (b t)"), banks
 
         w_codes = weights.tile([P, HALVES, BASES, OUTPUTS], U32, align_bytes=64)
         w_scales = weights.tile([P, HALVES, BASES, OUTPUTS], U8, align_bytes=64)
@@ -210,23 +210,24 @@ def tile_kanlayer_kernel(tc, x, knots, control_points, out):
                 in_=w_grouped[:].rearrange("p n o t -> p (n o t)"),
             )
 
-        def clamp_distance(dist, vg, i):
+        def clamp_distance(dist, v, i):
             on_right = i in P_ONLY
             nc.vector.tensor_scalar(
                 out=dist,
-                in0=vg,
+                in0=v[0],
                 scalar1=c["t"][:, i : i + 1],
                 scalar2=TINY if on_right else -TINY,
                 op0=ALU.subtract,
                 op1=ALU.max if on_right else ALU.min,
             )
 
-        def log_distance(dist, vg, i, clamp=False):
+        def log_distance(dist, v, i, clamp=False):
             if i == 0:
-                nc.scalar.activation(out=dist, in_=vg, func=ACT.Ln, bias=c["first_bias"][:])
+                nc.scalar.activation(out=dist, in_=v[0], func=ACT.Ln, bias=c["first_bias"][:])
             elif clamp:
+                sign, bias = (1.0, c["neg_t"]) if i in P_ONLY else (-1.0, c["t"])
                 nc.scalar.activation(
-                    out=dist, in_=vg, func=ACT.Relu, scale=-1.0, bias=c["t"][:, i : i + 1]
+                    out=dist, in_=v[0], func=ACT.Relu, scale=sign, bias=bias[:, i : i + 1]
                 )
                 nc.scalar.activation(out=dist, in_=dist, func=ACT.Ln, bias=c["tiny"][:])
             else:
@@ -245,29 +246,47 @@ def tile_kanlayer_kernel(tc, x, knots, control_points, out):
             pairs = [single_pool.tile([P, 2, CHUNK], F32, name="last%d" % n) for n in range(2)]
             return {i: pairs[(i - 10) // 2][:, i % 2, :] for i in Q_ONLY}
 
-        def make_square(vg, i):
+        def make_square(v, i):
             square = square_pool.tile([P, CHUNK], F32, name="square")
-            if i in (4, 9):
-                col = slice(0, 1) if i == 4 else slice(1, 2)
-                bias, scale = c["root_bias"][:, col], c["root"][:, col]
-            else:
-                bias, scale = c["neg_t"][:, i : i + 1], 1.0
-            nc.scalar.activation(out=square[:], in_=vg, func=ACT.Square, bias=bias, scale=scale)
+            nc.scalar.activation(
+                out=square[:],
+                in_=v[0],
+                func=ACT.Square,
+                bias=c["root_bias"][:, i - 4 : i - 3],
+                scale=c["root"][:, i - 4 : i - 3],
+            )
             return square
 
-        def negate(vg):
+        def negate(v):
             negated = stage.tile([P, CHUNK], BF16, name="right")
-            nc.vector.tensor_scalar_mul(out=negated[:], in0=vg, scalar1=-1.0)
+            nc.vector.tensor_scalar_mul(out=negated[:], in0=v[0], scalar1=-1.0)
             return negated[:]
 
-        def signed_cube(vg, i, square):
+        def bank_part(tile, n):
+            half = CHUNK // 2
+            return tile[:, n * half : (n + 1) * half].rearrange("p (b t) -> p b t", t=PACK)
+
+        def signed_cube(v, i, square):
+            cube = cube_pool.tile([P, CHUNK], F32, name="cube")
+            for n, bank in enumerate(v[1]):
+                nc.vector.scalar_tensor_tensor(
+                    out=bank_part(cube, n),
+                    in0=bank,
+                    scalar=c["t"][:, i : i + 1],
+                    in1=bank_part(square, n),
+                    op0=ALU.subtract,
+                    op1=ALU.mult,
+                )
+            return cube
+
+        def negated_cube(negated, i, square):
             cube = cube_pool.tile([P, CHUNK], F32, name="cube")
             nc.vector.scalar_tensor_tensor(
                 out=cube[:],
-                in0=vg,
+                in0=negated,
                 scalar=c["t"][:, i : i + 1],
                 in1=square[:],
-                op0=ALU.add if i == 9 else ALU.subtract,
+                op0=ALU.add,
                 op1=ALU.mult,
             )
             return cube
@@ -280,13 +299,24 @@ def tile_kanlayer_kernel(tc, x, knots, control_points, out):
             p_tile = (
                 edge_pool.tile([P, CHUNK], BF16, name="last_edge")
                 if i == 9
-                else side_pool.tile([P, CHUNK], F32, name="p_cube")
+                else p_pool.tile([P, CHUNK], F32, name="p_cube")
             )
-            p_side = relu_of(cube, c["p_side"][:, i - 4 : i - 3], p_tile)
+            if 6 <= i <= 8:
+                nc.gpsimd.tensor_scalar(
+                    out=p_tile[:],
+                    in0=cube[:],
+                    scalar1=BOUND,
+                    scalar2=0.0,
+                    op0=ALU.min,
+                    op1=ALU.max,
+                )
+                p_side = p_tile[:]
+            else:
+                p_side = relu_of(cube, c["p_side"][:, i - 4 : i - 3], p_tile)
             q_tile = (
                 edge_pool.tile([P, CHUNK], BF16, name="first_edge")
                 if i == 4
-                else side_pool.tile([P, CHUNK], F32, name="q_cube")
+                else q_pool.tile([P, CHUNK], F32, name="q_cube")
             )
             q_side = relu_of(cube, c["q_side"][:, i - 4 : i - 3], q_tile)
             return p_side, q_side
@@ -362,10 +392,8 @@ def tile_kanlayer_kernel(tc, x, knots, control_points, out):
         ident = consts.tile([P, P], BF16)
         make_identity(nc, ident[:])
 
-        v_now = new_values()
-        for m in range(ROW_TILES):
-            flip_tile(x_tiles[m], m, v_now, nc.vector.tensor_copy if m % 2 else nc.scalar.copy)
-        vg = flat(v_now[0])
+        v_after = flip_values(x_tiles, 0, (nc.scalar.copy, nc.vector.tensor_copy))
+        vg = v_after
         cube_next = {}
         square = make_square(vg, 4)
         square_after = make_square(vg, 5)
@@ -394,27 +422,26 @@ def tile_kanlayer_kernel(tc, x, knots, control_points, out):
         for r in range(ROUNDS):
             for g in range(HALVES):
                 final = r == ROUNDS - 1 and g == HALVES - 1
-                vg = flat(v_now[g])
+                vg = v_after
                 p_cube = dict(first)
                 q_cube = new_last()
                 cube = dict(cube_next)
                 left = {}
 
                 for i in BOTH:
-                    if i == 4 and g == HALVES - 1 and not final:
-                        v_now = new_values()
-                        for m in range(ROW_TILES):
-                            flip_tile(x_tiles[m], m, v_now, nc.scalar.copy)
-                    if i == 4:
-                        v_after = None if final else flat(v_now[(g + 1) % HALVES])
+                    if i == 4 and not final:
+                        v_after = flip_values(x_tiles, (g + 1) % HALVES, [nc.scalar.copy] * 2)
                     p_cube[i], q_cube[i] = sides
                     if i + 2 <= BOTH[-1]:
                         square_after = make_square(vg, i + 2)
                     elif not final:
                         square_after = make_square(v_after, i + 2 - len(BOTH))
                     if i < BOTH[-1]:
-                        source = negated if i + 1 == 9 else vg
-                        cube[i + 1] = signed_cube(source, i + 1, square)
+                        cube[i + 1] = (
+                            negated_cube(negated, i + 1, square)
+                            if i + 1 == 9
+                            else signed_cube(vg, i + 1, square)
+                        )
                         sides = make_sides(cube[i + 1], i + 1)
                     elif not final:
                         cube_next = {4: signed_cube(v_after, 4, square)}
@@ -423,10 +450,9 @@ def tile_kanlayer_kernel(tc, x, knots, control_points, out):
                     if waiting:
                         multiply(*waiting.pop())
 
-                    by_scalar = Q_ONLY if final else (13,)
-                    late = (12, 13) if final else (13,) if g == HALVES - 1 else ()
+                    by_scalar = Q_ONLY if final else (3, 11, 12, 13)
                     for n in Q_ONLY:
-                        if i == (5 if n in late else 4):
+                        if i == (5 if n == 13 else 4):
                             if n not in by_scalar:
                                 clamp_distance(q_cube[n], vg, n)
                             log_distance(q_cube[n], vg, n, clamp=n in by_scalar)
@@ -434,8 +460,8 @@ def tile_kanlayer_kernel(tc, x, knots, control_points, out):
                         if i == 5:
                             first = {n: new_first(n) for n in P_ONLY}
                         if 5 <= i <= 8:
-                            log_distance(first[i - 5], v_after, i - 5)
-                        if 5 <= i <= 7:
+                            log_distance(first[i - 5], v_after, i - 5, clamp=i - 5 in by_scalar)
+                        if 5 <= i <= 7 and i - 4 not in by_scalar:
                             clamp_distance(first[i - 4], v_after, i - 4)
                     if i == 8:
                         cube_distance(q_cube[10], 10)

@@ -97,8 +97,6 @@ def spline_constants(nc, pool, knots):
     nc.vector.tensor_copy(out=factor[:], in_=p_factor[:, 4 : 4 + both])
     nc.vector.tensor_mul(out=factor[:, 0:1], in0=q_factor[:, 1:2], in1=right_w[:, 1:2])
     nc.vector.tensor_scalar_mul(out=factor[:, 0:1], in0=factor[:, 0:1], scalar1=-1.0)
-    nc.vector.tensor_mul(out=factor[:, 5:6], in0=p_factor[:, 9:10], in1=left_w[:, 8:9])
-    nc.vector.tensor_scalar_mul(out=factor[:, 5:6], in0=factor[:, 5:6], scalar1=-1.0)
     half = pool.tile([P, both], F32)
     nc.gpsimd.memset(half[:], 0.5)
     root = pool.tile([P, both], F32)
@@ -107,10 +105,9 @@ def spline_constants(nc, pool, knots):
     nc.vector.tensor_mul(out=root_bias[:], in0=root[:], in1=neg_t[:, 4 : 4 + both])
     recip = pool.tile([P, both], F32)
     nc.vector.reciprocal(out=recip[:], in_=factor[:])
-    nc.vector.tensor_scalar_mul(out=recip[:, 5:6], in0=recip[:, 5:6], scalar1=-1.0)
 
-    p_side = pool.tile([P, both], F32)
-    nc.vector.tensor_mul(out=p_side[:], in0=p_factor[:, 4 : 4 + both], in1=recip[:])
+    p_side = pool.tile([P, 1], F32)
+    nc.vector.tensor_mul(out=p_side[:], in0=p_factor[:, 4:5], in1=recip[:, 0:1])
     q_side = pool.tile([P, both], F32)
     nc.vector.tensor_scalar_mul(out=q_side[:], in0=q_factor[:, 1 : 1 + both], scalar1=-1.0)
     nc.vector.tensor_mul(out=q_side[:], in0=q_side[:], in1=recip[:])
@@ -165,10 +162,9 @@ def tile_kanlayer_kernel(tc, x, knots, control_points, out):
                 tiles.append(x_sb)
             return tiles
 
-        def flip_values(x_tiles, g, copies):
-            v = v_pool.tile([P, ROWS, PACK], BF16, name="v")
+        def flip_values(x_tiles, g):
             banks = []
-            for pair, copy in enumerate(copies):
+            for pair in range(2):
                 bank = flip_psum.tile([P, PACK, 2 * P], BF16, name="flip")
                 for n in range(2):
                     for t in range(PACK):
@@ -177,9 +173,13 @@ def tile_kanlayer_kernel(tc, x, knots, control_points, out):
                             x_tiles[2 * pair + n][:, feature_columns(g * PACK + t)],
                             ident[:],
                         )
-                view = bank[:].rearrange("p t b -> p b t")
-                copy(out=v[:, 2 * pair * P : 2 * (pair + 1) * P, :], in_=view)
-                banks.append(view)
+                banks.append(bank[:].rearrange("p t b -> p b t"))
+            return banks
+
+        def copy_values(banks, copies):
+            v = v_pool.tile([P, ROWS, PACK], BF16, name="v")
+            for n, (bank, copy) in enumerate(zip(banks, copies)):
+                copy(out=v[:, 2 * n * P : 2 * (n + 1) * P, :], in_=bank)
             return v[:].rearrange("p b t -> p (b t)"), banks
 
         w_codes = weights.tile([P, HALVES, BASES, OUTPUTS], U32, align_bytes=64)
@@ -257,11 +257,6 @@ def tile_kanlayer_kernel(tc, x, knots, control_points, out):
             )
             return square
 
-        def negate(v):
-            negated = stage.tile([P, CHUNK], BF16, name="right")
-            nc.vector.tensor_scalar_mul(out=negated[:], in0=v[0], scalar1=-1.0)
-            return negated[:]
-
         def bank_part(tile, n):
             half = CHUNK // 2
             return tile[:, n * half : (n + 1) * half].rearrange("p (b t) -> p b t", t=PACK)
@@ -279,57 +274,34 @@ def tile_kanlayer_kernel(tc, x, knots, control_points, out):
                 )
             return cube
 
-        def negated_cube(negated, i, square):
-            cube = cube_pool.tile([P, CHUNK], F32, name="cube")
-            nc.vector.scalar_tensor_tensor(
-                out=cube[:],
-                in0=negated,
-                scalar=c["t"][:, i : i + 1],
-                in1=square[:],
-                op0=ALU.add,
-                op1=ALU.mult,
-            )
-            return cube
-
         def relu_of(cube, scale, tile):
             nc.scalar.activation(out=tile[:], in_=cube[:], func=ACT.Relu, scale=scale)
             return tile[:]
 
-        def make_sides(cube, i):
-            p_tile = (
-                edge_pool.tile([P, CHUNK], BF16, name="last_edge")
-                if i == 9
-                else p_pool.tile([P, CHUNK], F32, name="p_cube")
+        def make_p(cube, i):
+            side = p_pool.tile([P, CHUNK], F32, name="p_cube")
+            if i == 4:
+                return relu_of(cube, c["p_side"][:], side)
+            nc.gpsimd.tensor_scalar(
+                out=side[:],
+                in0=cube[:],
+                scalar1=BOUND,
+                scalar2=0.0,
+                op0=ALU.min,
+                op1=ALU.max,
             )
-            if 6 <= i <= 8:
-                nc.gpsimd.tensor_scalar(
-                    out=p_tile[:],
-                    in0=cube[:],
-                    scalar1=BOUND,
-                    scalar2=0.0,
-                    op0=ALU.min,
-                    op1=ALU.max,
-                )
-                p_side = p_tile[:]
+            return side[:]
+
+        def make_q(cube, i):
+            if i == 4:
+                side = edge_pool.tile([P, CHUNK], BF16, name="edge")
             else:
-                p_side = relu_of(cube, c["p_side"][:, i - 4 : i - 3], p_tile)
-            q_tile = (
-                edge_pool.tile([P, CHUNK], BF16, name="first_edge")
-                if i == 4
-                else q_pool.tile([P, CHUNK], F32, name="q_cube")
-            )
-            q_side = relu_of(cube, c["q_side"][:, i - 4 : i - 3], q_tile)
-            return p_side, q_side
+                side = q_pool.tile([P, CHUNK], F32, name="q_cube")
+            return relu_of(cube, c["q_side"][:, i - 4 : i - 3], side)
 
         def combine(out, in0, factor, in1):
             nc.vector.scalar_tensor_tensor(
                 out=out, in0=in0, scalar=factor, in1=in1, op0=ALU.mult, op1=ALU.add
-            )
-            return out
-
-        def add_negative(out, cube, in1):
-            nc.vector.scalar_tensor_tensor(
-                out=out, in0=cube[:], scalar=0.0, in1=in1, op0=ALU.min, op1=ALU.add
             )
             return out
 
@@ -341,14 +313,16 @@ def tile_kanlayer_kernel(tc, x, knots, control_points, out):
             right = stage.tile([P, CHUNK], BF16, name="right")
             return right[:]
 
-        def left_side(k, p_cube, cube):
-            if k == 8:
-                return add_negative(new_left(), cube[9], p_cube[8])
+        def left_side(k, p_cube):
             return combine(new_left(), p_cube[k + 1], c["left_w"][:, k : k + 1], p_cube[k])
 
         def right_side(k, q_cube, cube):
             if k == 1:
-                return add_negative(new_right(), cube[4], q_cube[5])
+                right = new_right()
+                nc.vector.scalar_tensor_tensor(
+                    out=right, in0=cube[4][:], scalar=0.0, in1=q_cube[5], op0=ALU.min, op1=ALU.add
+                )
+                return right
             return combine(new_right(), q_cube[k + 3], c["right_w"][:, k : k + 1], q_cube[k + 4])
 
         def join(one, other, op):
@@ -392,20 +366,18 @@ def tile_kanlayer_kernel(tc, x, knots, control_points, out):
         ident = consts.tile([P, P], BF16)
         make_identity(nc, ident[:])
 
-        v_after = flip_values(x_tiles, 0, (nc.scalar.copy, nc.vector.tensor_copy))
-        vg = v_after
-        cube_next = {}
-        square = make_square(vg, 4)
-        square_after = make_square(vg, 5)
+        v = copy_values(flip_values(x_tiles, 0), (nc.scalar.copy, nc.vector.tensor_copy))
+        square = make_square(v, 4)
+        square_after = make_square(v, 5)
         first = {i: new_first(i) for i in P_ONLY}
         for i in P_ONLY[1:]:
-            clamp_distance(first[i], vg, i)
+            clamp_distance(first[i], v, i)
         for i in P_ONLY:
-            log_distance(first[i], vg, i)
+            log_distance(first[i], v, i)
         for i in P_ONLY:
             cube_distance(first[i], i)
-        cube_next[4] = signed_cube(vg, 4, square)
-        sides = make_sides(cube_next[4], 4)
+        cube = {4: signed_cube(v, 4, square)}
+        p_four, q_four = make_p(cube[4], 4), make_q(cube[4], 4)
         square = square_after
         grouped = None
         for g in range(HALVES):
@@ -415,47 +387,55 @@ def tile_kanlayer_kernel(tc, x, knots, control_points, out):
                     quantise_weights(*grouped)
                 grouped = (w_grouped, g, k)
         quantise_weights(*grouped)
-        negated = None
+        banks = flip_values(x_tiles, 1)
 
         acc = new_sums()
         waiting = []
+
+        def quantise_waiting():
+            if waiting:
+                multiply(*waiting.pop())
+
         for r in range(ROUNDS):
             for g in range(HALVES):
                 final = r == ROUNDS - 1 and g == HALVES - 1
-                vg = v_after
+                by_scalar = Q_ONLY if final else (11, 12, 13)
                 p_cube = dict(first)
                 q_cube = new_last()
-                cube = dict(cube_next)
+                p_cube[4], q_cube[4] = p_four, q_four
+                cube = {4: cube[4]}
                 left = {}
 
                 for i in BOTH:
-                    if i == 4 and not final:
-                        v_after = flip_values(x_tiles, (g + 1) % HALVES, [nc.scalar.copy] * 2)
-                    p_cube[i], q_cube[i] = sides
                     if i + 2 <= BOTH[-1]:
-                        square_after = make_square(vg, i + 2)
+                        square_after = make_square(v, i + 2)
                     elif not final:
                         square_after = make_square(v_after, i + 2 - len(BOTH))
-                    if i < BOTH[-1]:
-                        cube[i + 1] = (
-                            negated_cube(negated, i + 1, square)
-                            if i + 1 == 9
-                            else signed_cube(vg, i + 1, square)
-                        )
-                        sides = make_sides(cube[i + 1], i + 1)
+                    if i == 4:
+                        cube[5] = signed_cube(v, 5, square)
+                        cube[6] = signed_cube(v, 6, square_after)
+                        p_cube[5] = make_p(cube[5], 5)
+                        q_cube[5] = make_q(cube[5], 5)
+                    elif i == 5:
+                        p_cube[6] = make_p(cube[6], 6)
+                        q_cube[6] = make_q(cube[6], 6)
+                    elif i < BOTH[-1]:
+                        cube[i + 1] = signed_cube(v, i + 1, square)
+                        p_cube[i + 1] = make_p(cube[i + 1], i + 1)
+                        q_cube[i + 1] = make_q(cube[i + 1], i + 1)
                     elif not final:
-                        cube_next = {4: signed_cube(v_after, 4, square)}
-                        sides = make_sides(cube_next[4], 4)
+                        cube[4] = signed_cube(v_after, 4, square)
+                        q_four = make_q(cube[4], 4)
                     square = square_after
-                    if waiting:
-                        multiply(*waiting.pop())
+                    quantise_waiting()
 
-                    by_scalar = Q_ONLY if final else (3, 11, 12, 13)
+                    if i == 4 and not final:
+                        v_after = copy_values(banks, [nc.scalar.copy] * 2)
                     for n in Q_ONLY:
                         if i == (5 if n == 13 else 4):
                             if n not in by_scalar:
-                                clamp_distance(q_cube[n], vg, n)
-                            log_distance(q_cube[n], vg, n, clamp=n in by_scalar)
+                                clamp_distance(q_cube[n], v, n)
+                            log_distance(q_cube[n], v, n, clamp=n in by_scalar)
                     if not final:
                         if i == 5:
                             first = {n: new_first(n) for n in P_ONLY}
@@ -466,12 +446,8 @@ def tile_kanlayer_kernel(tc, x, knots, control_points, out):
                     if i == 8:
                         cube_distance(q_cube[10], 10)
                     if i == 9:
-                        cube_distance(q_cube[11], 11)
-                        cube_distance(q_cube[12], 12)
-                        cube_distance(q_cube[13], 13)
-                        if not final:
-                            for n in P_ONLY:
-                                cube_distance(first[n], n)
+                        for n in Q_ONLY[1:]:
+                            cube_distance(q_cube[n], n)
 
                     if i == 4 and g == 0 and r > 0:
                         store_result(r - 1, acc)
@@ -481,28 +457,34 @@ def tile_kanlayer_kernel(tc, x, knots, control_points, out):
 
                     if i == 4:
                         two = combine(p_cube[0], p_cube[1], c["left_w"][:, 0:1], p_cube[0])
-                        left[1] = left_side(1, p_cube, cube)
+                        left[1] = left_side(1, p_cube)
                         three = combine(new_right(), p_cube[2], c["third_w"][:, 0:1], two)
-                        left[2] = left_side(2, p_cube, cube)
-                        left[3] = left_side(3, p_cube, cube)
+                        left[2] = left_side(2, p_cube)
+                        left[3] = left_side(3, p_cube)
                         waiting.append((join(three, q_cube[4], ALU.min), 0, g, acc))
                     else:
                         k = i - 4
                         right = right_side(k, q_cube, cube)
-                        left[i - 1] = left_side(i - 1, p_cube, cube)
-                        if i == 7:
-                            negated = negate(vg)
+                        left[i - 1] = left_side(i - 1, p_cube)
                         waiting.append((join(left[k], right, ALU.max), k, g, acc))
+                    if i == 9 and not final:
+                        p_four = make_p(cube[4], 4)
+                        for n in P_ONLY:
+                            cube_distance(first[n], n)
 
                 for k in (6, 7, 8):
                     right = right_side(k, q_cube, cube)
-                    multiply(*waiting.pop())
+                    quantise_waiting()
                     waiting.append((join(left[k], right, ALU.max), k, g, acc))
                     if k == 7:
                         two = combine(q_cube[13], q_cube[12], c["right_w"][:, 9:10], q_cube[13])
                 three = combine(new_right(), q_cube[11], c["third_w"][:, 1:2], two)
-                multiply(*waiting.pop())
+                quantise_waiting()
                 waiting.append((join(three, p_cube[9], ALU.min), 9, g, acc))
+                if not final:
+                    v = v_after
+                    if r < ROUNDS - 1:
+                        banks = flip_values(x_tiles, g)
 
-        multiply(*waiting.pop())
+        quantise_waiting()
         store_result(ROUNDS - 1, acc)

@@ -221,14 +221,16 @@ def tile_kanlayer_kernel(tc, x, knots, control_points, out):
                 op1=ALU.max if on_right else ALU.min,
             )
 
+        def clamp_on_scalar(dist, v, i):
+            sign, bias = (1.0, c["neg_t"]) if i in P_ONLY else (-1.0, c["t"])
+            nc.scalar.activation(
+                out=dist, in_=v[0], func=ACT.Relu, scale=sign, bias=bias[:, i : i + 1]
+            )
+
         def log_distance(dist, v, i, clamp=False):
             if i == 0:
                 nc.scalar.activation(out=dist, in_=v[0], func=ACT.Ln, bias=c["first_bias"][:])
             elif clamp:
-                sign, bias = (1.0, c["neg_t"]) if i in P_ONLY else (-1.0, c["t"])
-                nc.scalar.activation(
-                    out=dist, in_=v[0], func=ACT.Relu, scale=sign, bias=bias[:, i : i + 1]
-                )
                 nc.scalar.activation(out=dist, in_=dist, func=ACT.Ln, bias=c["tiny"][:])
             else:
                 sign = 1.0 if i in P_ONLY else -1.0
@@ -366,19 +368,17 @@ def tile_kanlayer_kernel(tc, x, knots, control_points, out):
         ident = consts.tile([P, P], BF16)
         make_identity(nc, ident[:])
 
-        v = copy_values(flip_values(x_tiles, 0), (nc.scalar.copy, nc.vector.tensor_copy))
-        square = make_square(v, 4)
-        square_after = make_square(v, 5)
+        v = copy_values(flip_values(x_tiles, 0), [nc.scalar.copy] * 2)
+        square = {4: make_square(v, 4), 5: make_square(v, 5)}
         first = {i: new_first(i) for i in P_ONLY}
         for i in P_ONLY[1:]:
             clamp_distance(first[i], v, i)
         for i in P_ONLY:
             log_distance(first[i], v, i)
+        cube = {4: signed_cube(v, 4, square[4])}
+        square[6] = make_square(v, 6)
         for i in P_ONLY:
             cube_distance(first[i], i)
-        cube = {4: signed_cube(v, 4, square)}
-        p_four, q_four = make_p(cube[4], 4), make_q(cube[4], 4)
-        square = square_after
         grouped = None
         for g in range(HALVES):
             for k in range(0, BASES, 2):
@@ -399,50 +399,53 @@ def tile_kanlayer_kernel(tc, x, knots, control_points, out):
         for r in range(ROUNDS):
             for g in range(HALVES):
                 final = r == ROUNDS - 1 and g == HALVES - 1
-                by_scalar = Q_ONLY if final else (11, 12, 13)
+                by_scalar = Q_ONLY if final else (13,) if r == 0 and g == 0 else (3, 11, 12, 13)
                 p_cube = dict(first)
                 q_cube = new_last()
-                p_cube[4], q_cube[4] = p_four, q_four
                 cube = {4: cube[4]}
                 left = {}
 
                 for i in BOTH:
-                    if i + 2 <= BOTH[-1]:
-                        square_after = make_square(v, i + 2)
-                    elif not final:
-                        square_after = make_square(v_after, i + 2 - len(BOTH))
+                    if 5 <= i <= 7:
+                        square[i + 2] = make_square(v, i + 2)
+                    elif i >= 8 and not final:
+                        square[i - 4] = make_square(v_after, i - 4)
                     if i == 4:
-                        cube[5] = signed_cube(v, 5, square)
-                        cube[6] = signed_cube(v, 6, square_after)
+                        p_cube[4] = make_p(cube[4], 4)
+                        q_cube[4] = make_q(cube[4], 4)
+                        cube[5] = signed_cube(v, 5, square[5])
+                        cube[6] = signed_cube(v, 6, square[6])
                         p_cube[5] = make_p(cube[5], 5)
-                        q_cube[5] = make_q(cube[5], 5)
                     elif i == 5:
                         p_cube[6] = make_p(cube[6], 6)
                         q_cube[6] = make_q(cube[6], 6)
                     elif i < BOTH[-1]:
-                        cube[i + 1] = signed_cube(v, i + 1, square)
+                        cube[i + 1] = signed_cube(v, i + 1, square[i + 1])
                         p_cube[i + 1] = make_p(cube[i + 1], i + 1)
                         q_cube[i + 1] = make_q(cube[i + 1], i + 1)
                     elif not final:
-                        cube[4] = signed_cube(v_after, 4, square)
-                        q_four = make_q(cube[4], 4)
-                    square = square_after
+                        cube[4] = signed_cube(v_after, 4, square[4])
                     quantise_waiting()
 
                     if i == 4 and not final:
                         v_after = copy_values(banks, [nc.scalar.copy] * 2)
-                    for n in Q_ONLY:
-                        if i == (5 if n == 13 else 4):
-                            if n not in by_scalar:
-                                clamp_distance(q_cube[n], v, n)
-                            log_distance(q_cube[n], v, n, clamp=n in by_scalar)
-                    if not final:
-                        if i == 5:
-                            first = {n: new_first(n) for n in P_ONLY}
-                        if 5 <= i <= 8:
-                            log_distance(first[i - 5], v_after, i - 5, clamp=i - 5 in by_scalar)
-                        if 5 <= i <= 7 and i - 4 not in by_scalar:
-                            clamp_distance(first[i - 4], v_after, i - 4)
+                    knots = (10, 11, 12) if i == 4 else (13,) if i == 5 else ()
+                    for n in knots:
+                        (clamp_on_scalar if n in by_scalar else clamp_distance)(q_cube[n], v, n)
+                    if i == 4:
+                        q_cube[5] = make_q(cube[5], 5)
+                    if i == 5 and not final:
+                        first = {n: new_first(n) for n in P_ONLY}
+                        log_distance(first[0], v_after, 0)
+                    for n in knots:
+                        log_distance(q_cube[n], v, n, clamp=n in by_scalar)
+                    if 6 <= i <= 8 and not final:
+                        log_distance(first[i - 5], v_after, i - 5, clamp=i - 5 in by_scalar)
+                    if 5 <= i <= 7 and not final:
+                        n = i - 4
+                        (clamp_on_scalar if n in by_scalar else clamp_distance)(
+                            first[n], v_after, n
+                        )
                     if i == 8:
                         cube_distance(q_cube[10], 10)
                     if i == 9:
@@ -468,7 +471,7 @@ def tile_kanlayer_kernel(tc, x, knots, control_points, out):
                         left[i - 1] = left_side(i - 1, p_cube)
                         waiting.append((join(left[k], right, ALU.max), k, g, acc))
                     if i == 9 and not final:
-                        p_four = make_p(cube[4], 4)
+                        square[6] = make_square(v_after, 6)
                         for n in P_ONLY:
                             cube_distance(first[n], n)
 

@@ -137,11 +137,11 @@ def tile_kanlayer_kernel(tc, x, knots, control_points, out):
         weights = ctx.enter_context(tc.tile_pool(name="weights", bufs=1))
         x_pool = ctx.enter_context(tc.tile_pool(name="x_pool", bufs=ROW_TILES))
         v_pool = ctx.enter_context(tc.tile_pool(name="v_pool", bufs=2))
-        stage = ctx.enter_context(tc.tile_pool(name="stage", bufs=2))
+        right_pool = ctx.enter_context(tc.tile_pool(name="right_pool", bufs=2))
         result_pool = ctx.enter_context(tc.tile_pool(name="result_pool", bufs=1))
         single_pool = ctx.enter_context(tc.tile_pool(name="single_pool", bufs=1))
         square_pool = ctx.enter_context(tc.tile_pool(name="square_pool", bufs=2))
-        cube_pool = ctx.enter_context(tc.tile_pool(name="cube_pool", bufs=3))
+        cube_pool = ctx.enter_context(tc.tile_pool(name="cube_pool", bufs=4))
         p_pool = ctx.enter_context(tc.tile_pool(name="p_pool", bufs=2))
         q_pool = ctx.enter_context(tc.tile_pool(name="q_pool", bufs=3))
         edge_pool = ctx.enter_context(tc.tile_pool(name="edge_pool", bufs=1))
@@ -199,7 +199,9 @@ def tile_kanlayer_kernel(tc, x, knots, control_points, out):
                     nc.tensor.transpose(
                         w_flip[:, n, t, :], cp_sb[:, feature_columns(t), k + n], ident[:]
                     )
-            w_grouped = stage.tile([P, 2, OUTPUTS, PACK], BF16, name="w_grouped", align_bytes=64)
+            w_grouped = right_pool.tile(
+                [P, 2, OUTPUTS, PACK], BF16, name="right", align_bytes=64
+            )
             nc.vector.tensor_copy(out=w_grouped[:], in_=w_flip[:].rearrange("p n t o -> p n o t"))
             return w_grouped
 
@@ -294,6 +296,13 @@ def tile_kanlayer_kernel(tc, x, knots, control_points, out):
             )
             return side[:]
 
+        def make_edge(cube):
+            side = right_pool.tile([P, CHUNK], BF16, name="right", align_bytes=64)
+            nc.gpsimd.tensor_scalar(
+                out=side[:], in0=cube[:], scalar1=BOUND, scalar2=0.0, op0=ALU.min, op1=ALU.max
+            )
+            return side[:]
+
         def make_q(cube, i):
             if i == 4:
                 side = edge_pool.tile([P, CHUNK], BF16, name="edge")
@@ -312,7 +321,7 @@ def tile_kanlayer_kernel(tc, x, knots, control_points, out):
             return left[:]
 
         def new_right():
-            right = stage.tile([P, CHUNK], BF16, name="right")
+            right = right_pool.tile([P, CHUNK], BF16, name="right", align_bytes=64)
             return right[:]
 
         def left_side(k, p_cube):
@@ -396,6 +405,11 @@ def tile_kanlayer_kernel(tc, x, knots, control_points, out):
             if waiting:
                 multiply(*waiting.pop())
 
+        def join_last(three, edge, g, acc):
+            waiting.append((join(three, edge, ALU.min), 9, g, acc))
+
+        last = None
+
         for r in range(ROUNDS):
             for g in range(HALVES):
                 final = r == ROUNDS - 1 and g == HALVES - 1
@@ -426,6 +440,8 @@ def tile_kanlayer_kernel(tc, x, knots, control_points, out):
                     elif not final:
                         cube[4] = signed_cube(v_after, 4, square[4])
                     quantise_waiting()
+                    if i == 4 and last:
+                        join_last(*last)
 
                     if i == 4 and not final:
                         v_after = copy_values(banks, [nc.scalar.copy] * 2)
@@ -452,14 +468,15 @@ def tile_kanlayer_kernel(tc, x, knots, control_points, out):
                         for n in Q_ONLY[1:]:
                             cube_distance(q_cube[n], n)
 
-                    if i == 4 and g == 0 and r > 0:
-                        store_result(r - 1, acc)
-                        acc = new_sums()
                     if i == 5 and g == 0 and r < ROUNDS - 1:
                         x_tiles = load_rows(r + 1)
 
                     if i == 4:
                         two = combine(p_cube[0], p_cube[1], c["left_w"][:, 0:1], p_cube[0])
+                        quantise_waiting()
+                        if g == 0 and r > 0:
+                            store_result(r - 1, acc)
+                            acc = new_sums()
                         left[1] = left_side(1, p_cube)
                         three = combine(new_right(), p_cube[2], c["third_w"][:, 0:1], two)
                         left[2] = left_side(2, p_cube)
@@ -475,19 +492,22 @@ def tile_kanlayer_kernel(tc, x, knots, control_points, out):
                         for n in P_ONLY:
                             cube_distance(first[n], n)
 
-                for k in (6, 7, 8):
+                for k in (6, 7):
                     right = right_side(k, q_cube, cube)
                     quantise_waiting()
                     waiting.append((join(left[k], right, ALU.max), k, g, acc))
-                    if k == 7:
-                        two = combine(q_cube[13], q_cube[12], c["right_w"][:, 9:10], q_cube[13])
-                three = combine(new_right(), q_cube[11], c["third_w"][:, 1:2], two)
+                two = combine(q_cube[13], q_cube[12], c["right_w"][:, 9:10], q_cube[13])
+                right = right_side(8, q_cube, cube)
                 quantise_waiting()
-                waiting.append((join(three, p_cube[9], ALU.min), 9, g, acc))
+                three = combine(new_right(), q_cube[11], c["third_w"][:, 1:2], two)
+                waiting.append((join(left[8], right, ALU.max), 8, g, acc))
+                last = (three, make_edge(cube[9]), g, acc)
                 if not final:
                     v = v_after
                     if r < ROUNDS - 1:
                         banks = flip_values(x_tiles, g)
 
+        quantise_waiting()
+        join_last(*last)
         quantise_waiting()
         store_result(ROUNDS - 1, acc)

@@ -26,11 +26,14 @@ ROW_TILES = ROWS // P
 ROUNDS = BATCH // ROWS
 CHUNK = ROWS * PACK
 BOUND = 2.0**100
+STEP = 2.0**-24
 TINY = 2.0**-60
 
 P_ONLY = (0, 1, 2, 3)
 BOTH = (4, 5, 6, 7, 8, 9)
 Q_ONLY = (10, 11, 12, 13)
+ON_GPSIMD = (10, 11, 12, 13)
+BY_ROWS = (0, 2, 11, 13)
 
 FLOPS = 2 * BATCH * BASES * FEATURES * OUTPUTS
 
@@ -68,8 +71,6 @@ def spline_constants(nc, pool, knots):
     nc.vector.tensor_mul(out=q_prod[:], in0=q_prod[:], in1=d3[:, 0:cubes])
     q_factor = pool.tile([P, cubes], F32)
     nc.vector.reciprocal(out=q_factor[:], in_=q_prod[:])
-    p_log = pool.tile([P, cubes], F32)
-    nc.scalar.activation(out=p_log[:], in_=p_factor[:], func=ACT.Ln)
     q_log = pool.tile([P, cubes], F32)
     nc.scalar.activation(out=q_log[:], in_=q_factor[:], func=ACT.Ln)
 
@@ -92,9 +93,22 @@ def spline_constants(nc, pool, knots):
     nc.vector.reciprocal(out=third_recip[:], in_=third_den[:])
     nc.vector.tensor_mul(out=third_w[:], in0=third_w[:], in1=third_recip[:])
 
+    norm = pool.tile([P, BASES], F32)
+    nc.vector.memset(norm[:], 1.0)
+    nc.vector.tensor_copy(out=norm[:, 2:3], in_=third_w[:, 0:1])
+    nc.vector.tensor_scalar_mul(out=norm[:, 3:BASES], in0=left_w[:, 2 : BASES - 1], scalar1=-1.0)
+    left_scale = pool.tile([P, BASES], F32)
+    nc.vector.reciprocal(out=left_scale[:], in_=norm[:])
+    second_w = pool.tile([P, 1], F32)
+    nc.vector.tensor_mul(out=second_w[:], in0=left_w[:, 1:2], in1=left_scale[:, 2:3])
+    p_normed = pool.tile([P, BASES], F32)
+    nc.vector.tensor_mul(out=p_normed[:], in0=p_factor[:, 0:BASES], in1=norm[:])
+    p_log = pool.tile([P, BASES], F32)
+    nc.scalar.activation(out=p_log[:], in_=p_normed[:], func=ACT.Ln)
+
     both = len(BOTH)
     factor = pool.tile([P, both], F32)
-    nc.vector.tensor_copy(out=factor[:], in_=p_factor[:, 4 : 4 + both])
+    nc.vector.tensor_copy(out=factor[:], in_=p_normed[:, 4 : 4 + both])
     nc.vector.tensor_mul(out=factor[:, 0:1], in0=q_factor[:, 1:2], in1=right_w[:, 1:2])
     nc.vector.tensor_scalar_mul(out=factor[:, 0:1], in0=factor[:, 0:1], scalar1=-1.0)
     half = pool.tile([P, both], F32)
@@ -107,14 +121,17 @@ def spline_constants(nc, pool, knots):
     nc.vector.reciprocal(out=recip[:], in_=factor[:])
 
     p_side = pool.tile([P, 1], F32)
-    nc.vector.tensor_mul(out=p_side[:], in0=p_factor[:, 4:5], in1=recip[:, 0:1])
+    nc.vector.tensor_mul(out=p_side[:], in0=p_normed[:, 4:5], in1=recip[:, 0:1])
     q_side = pool.tile([P, both], F32)
     nc.vector.tensor_scalar_mul(out=q_side[:], in0=q_factor[:, 1 : 1 + both], scalar1=-1.0)
     nc.vector.tensor_mul(out=q_side[:], in0=q_side[:], in1=recip[:])
     tiny = pool.tile([P, 1], F32)
     nc.vector.memset(tiny[:], TINY)
+    below_t = pool.tile([P, KNOTS], F32)
+    nc.vector.tensor_scalar_add(out=below_t[:], in0=t[:], scalar1=-STEP)
     return {
         "t": t,
+        "below_t": below_t,
         "neg_t": neg_t,
         "first_bias": first_bias,
         "tiny": tiny,
@@ -123,6 +140,8 @@ def spline_constants(nc, pool, knots):
         "left_w": left_w,
         "right_w": right_w,
         "third_w": third_w,
+        "left_scale": left_scale,
+        "second_w": second_w,
         "root": root,
         "root_bias": root_bias,
         "p_side": p_side,
@@ -135,9 +154,9 @@ def tile_kanlayer_kernel(tc, x, knots, control_points, out):
     with ExitStack() as ctx:
         consts = ctx.enter_context(tc.tile_pool(name="consts", bufs=1))
         weights = ctx.enter_context(tc.tile_pool(name="weights", bufs=1))
-        x_pool = ctx.enter_context(tc.tile_pool(name="x_pool", bufs=ROW_TILES))
+        x_pool = ctx.enter_context(tc.tile_pool(name="x_pool", bufs=2))
         v_pool = ctx.enter_context(tc.tile_pool(name="v_pool", bufs=2))
-        right_pool = ctx.enter_context(tc.tile_pool(name="right_pool", bufs=2))
+        right_pool = ctx.enter_context(tc.tile_pool(name="right_pool", bufs=3))
         result_pool = ctx.enter_context(tc.tile_pool(name="result_pool", bufs=1))
         single_pool = ctx.enter_context(tc.tile_pool(name="single_pool", bufs=1))
         square_pool = ctx.enter_context(tc.tile_pool(name="square_pool", bufs=2))
@@ -148,21 +167,22 @@ def tile_kanlayer_kernel(tc, x, knots, control_points, out):
         left_pool = ctx.enter_context(tc.tile_pool(name="left_pool", bufs=5))
         mx_pool = ctx.enter_context(tc.tile_pool(name="mx_pool", bufs=2))
         flip_psum = ctx.enter_context(tc.psum_pool(name="flip_psum", bufs=4))
+        sum_psum = ctx.enter_context(tc.psum_pool(name="sum_psum", bufs=3))
         acc_psum = ctx.enter_context(tc.psum_pool(name="acc_psum", bufs=1))
         ctx.enter_context(
             tc.manual_schedule(engines={mybir.EngineType.Activation, mybir.EngineType.DVE})
         )
 
-        def load_rows(r):
-            tiles = []
+        def load_chunk(r, g):
+            x_sb = x_pool.tile([P, ROW_TILES, PASS], BF16, name="x_sb")
             for m in range(ROW_TILES):
-                x_sb = x_pool.tile([P, FEATURES], BF16, name="x_sb")
-                first = r * ROWS + m * P
-                nc.sync.dma_start(out=x_sb[:], in_=x[first : first + P, :])
-                tiles.append(x_sb)
-            return tiles
+                row = r * ROWS + m * P
+                nc.sync.dma_start(
+                    out=x_sb[:, m, :], in_=x[row : row + P, g * PASS : (g + 1) * PASS]
+                )
+            return x_sb
 
-        def flip_values(x_tiles, g):
+        def flip_values(x_sb):
             banks = []
             for pair in range(2):
                 bank = flip_psum.tile([P, PACK, 2 * P], BF16, name="flip")
@@ -170,17 +190,18 @@ def tile_kanlayer_kernel(tc, x, knots, control_points, out):
                     for t in range(PACK):
                         nc.tensor.transpose(
                             bank[:, t, n * P : (n + 1) * P],
-                            x_tiles[2 * pair + n][:, feature_columns(g * PACK + t)],
+                            x_sb[:, 2 * pair + n, feature_columns(t)],
                             ident[:],
                         )
                 banks.append(bank[:].rearrange("p t b -> p b t"))
-            return banks
+            return banks, x_sb[:].rearrange("p m (q t) -> p m t q", t=PACK)
 
-        def copy_values(banks, copies):
+        def copy_values(flipped):
+            banks, by_rows = flipped
             v = v_pool.tile([P, ROWS, PACK], BF16, name="v")
-            for n, (bank, copy) in enumerate(zip(banks, copies)):
-                copy(out=v[:, 2 * n * P : 2 * (n + 1) * P, :], in_=bank)
-            return v[:].rearrange("p b t -> p (b t)"), banks
+            for n, bank in enumerate(banks):
+                nc.scalar.copy(out=v[:, 2 * n * P : 2 * (n + 1) * P, :], in_=bank)
+            return v[:].rearrange("p b t -> p (b t)"), banks, by_rows
 
         w_codes = weights.tile([P, HALVES, BASES, OUTPUTS], U32, align_bytes=64)
         w_scales = weights.tile([P, HALVES, BASES, OUTPUTS], U8, align_bytes=64)
@@ -212,11 +233,28 @@ def tile_kanlayer_kernel(tc, x, knots, control_points, out):
                 in_=w_grouped[:].rearrange("p n o t -> p (n o t)"),
             )
 
+        def operands(dist, v, i):
+            if i in BY_ROWS:
+                return dist.rearrange("p (m t q) -> p m t q", m=ROW_TILES, t=PACK), v[2]
+            return dist, v[0]
+
+        def clamp_on_gpsimd(dist, v, i):
+            out, values = operands(dist, v, i)
+            nc.gpsimd.tensor_scalar(
+                out=out,
+                in0=values,
+                scalar1=c["below_t"][:, i : i + 1],
+                scalar2=-BOUND,
+                op0=ALU.min,
+                op1=ALU.max,
+            )
+
         def clamp_distance(dist, v, i):
             on_right = i in P_ONLY
+            out, values = operands(dist, v, i)
             nc.vector.tensor_scalar(
-                out=dist,
-                in0=v[0],
+                out=out,
+                in0=values,
                 scalar1=c["t"][:, i : i + 1],
                 scalar2=TINY if on_right else -TINY,
                 op0=ALU.subtract,
@@ -225,14 +263,20 @@ def tile_kanlayer_kernel(tc, x, knots, control_points, out):
 
         def clamp_on_scalar(dist, v, i):
             sign, bias = (1.0, c["neg_t"]) if i in P_ONLY else (-1.0, c["t"])
+            out, values = operands(dist, v, i)
             nc.scalar.activation(
-                out=dist, in_=v[0], func=ACT.Relu, scale=sign, bias=bias[:, i : i + 1]
+                out=out, in_=values, func=ACT.Relu, scale=sign, bias=bias[:, i : i + 1]
             )
 
-        def log_distance(dist, v, i, clamp=False):
+        def log_distance(dist, v, i, clamp):
             if i == 0:
-                nc.scalar.activation(out=dist, in_=v[0], func=ACT.Ln, bias=c["first_bias"][:])
-            elif clamp:
+                out, values = operands(dist, v, i)
+                nc.scalar.activation(out=out, in_=values, func=ACT.Ln, bias=c["first_bias"][:])
+            elif clamp is clamp_on_gpsimd:
+                nc.scalar.activation(
+                    out=dist, in_=dist, func=ACT.Ln, scale=-1.0, bias=c["t"][:, i : i + 1]
+                )
+            elif clamp is clamp_on_scalar:
                 nc.scalar.activation(out=dist, in_=dist, func=ACT.Ln, bias=c["tiny"][:])
             else:
                 sign = 1.0 if i in P_ONLY else -1.0
@@ -297,11 +341,8 @@ def tile_kanlayer_kernel(tc, x, knots, control_points, out):
             return side[:]
 
         def make_edge(cube):
-            side = right_pool.tile([P, CHUNK], BF16, name="right", align_bytes=64)
-            nc.gpsimd.tensor_scalar(
-                out=side[:], in0=cube[:], scalar1=BOUND, scalar2=0.0, op0=ALU.min, op1=ALU.max
-            )
-            return side[:]
+            edge = left_pool.tile([P, CHUNK], BF16, name="left")
+            return relu_of(cube, c["left_scale"][:, 9:10], edge)
 
         def make_q(cube, i):
             if i == 4:
@@ -310,9 +351,15 @@ def tile_kanlayer_kernel(tc, x, knots, control_points, out):
                 side = q_pool.tile([P, CHUNK], F32, name="q_cube")
             return relu_of(cube, c["q_side"][:, i - 4 : i - 3], side)
 
-        def combine(out, in0, factor, in1):
+        def combine(out, in0, weight, in1):
             nc.vector.scalar_tensor_tensor(
-                out=out, in0=in0, scalar=factor, in1=in1, op0=ALU.mult, op1=ALU.add
+                out=out, in0=in0, scalar=weight, in1=in1, op0=ALU.mult, op1=ALU.add
+            )
+            return out
+
+        def difference(out, in0, weight, in1):
+            nc.vector.scalar_tensor_tensor(
+                out=out, in0=in0, scalar=weight, in1=in1, op0=ALU.mult, op1=ALU.subtract
             )
             return out
 
@@ -325,7 +372,69 @@ def tile_kanlayer_kernel(tc, x, knots, control_points, out):
             return right[:]
 
         def left_side(k, p_cube):
-            return combine(new_left(), p_cube[k + 1], c["left_w"][:, k : k + 1], p_cube[k])
+            return difference(new_left(), p_cube[k], c["left_scale"][:, k : k + 1], p_cube[k + 1])
+
+        def row_tile_columns(m, t):
+            return slice((m * PACK + t) * P, (m * PACK + t + 1) * P)
+
+        def turn(cube, m, bank, t, start=True, stop=True):
+            nc.tensor.matmul(
+                bank[:, t, :],
+                lhsT=cube[:, row_tile_columns(m, t)],
+                rhs=ident_f32[:],
+                is_transpose=True,
+                start=start,
+                stop=stop,
+            )
+
+        def new_bank():
+            bank = sum_psum.tile([P, PACK, P], F32, name="sum")
+            return bank
+
+        def turn_one(cube, m):
+            bank = new_bank()
+            for t in range(PACK):
+                turn(cube, m, bank, t)
+            return bank[:].rearrange("p t b -> p b t")
+
+        def turn_first_sum(p_cube, m):
+            bank = new_bank()
+            for t in range(PACK):
+                turn(p_cube[2], m, bank, t, stop=False)
+                turn(p_cube[0], m, bank, t, start=False)
+            return bank[:].rearrange("p t b -> p b t")
+
+        def turn_last_sum(q_cube, m):
+            bank = new_bank()
+            for t in range(PACK):
+                nc.tensor.matmul(
+                    bank[:, t, :],
+                    lhsT=q_cube[11][:, row_tile_columns(m, t)],
+                    rhs=third_ident[:],
+                    start=True,
+                    stop=False,
+                )
+                turn(q_cube[13], m, bank, t, start=False)
+            return bank[:].rearrange("p t b -> p b t")
+
+        def row_tile(row, m):
+            return row[:, m * PACK * P : (m + 1) * PACK * P].rearrange("p (b t) -> p b t", t=PACK)
+
+        def use_second(m, bank, p_cube, left):
+            combine(row_tile(left[1], m), bank, c["second_w"][:], row_tile(p_cube[1], m))
+            difference(
+                row_tile(left[2], m), bank, c["left_scale"][:, 2:3], row_tile(p_cube[3], m)
+            )
+
+        def use_first_sum(m, bank, p_cube, three):
+            combine(row_tile(three, m), row_tile(p_cube[1], m), c["left_w"][:, 0:1], bank)
+
+        def use_eleventh(m, bank, q_cube, right):
+            combine(row_tile(right[7], m), row_tile(q_cube[10], m), c["right_w"][:, 7:8], bank)
+            combine(row_tile(right[8], m), bank, c["right_w"][:, 8:9], row_tile(q_cube[12], m))
+
+        def use_last_sum(m, bank, q_cube, three):
+            combine(row_tile(three, m), row_tile(q_cube[12], m), c["right_w"][:, 9:10], bank)
 
         def right_side(k, q_cube, cube):
             if k == 1:
@@ -347,73 +456,95 @@ def tile_kanlayer_kernel(tc, x, knots, control_points, out):
             nc.vector.quantize_mx(
                 out=b_codes[:].bitcast(FP8X4), scales=b_scales[:], in_=basis[:]
             )
-            for m in range(ROW_TILES):
-                b_cols = slice(m * P, (m + 1) * P)
-                nc.tensor.matmul_mx(
-                    out=acc[m][:],
-                    lhsT=b_codes[:, b_cols].bitcast(FP8X4),
-                    lhsT_scale=b_scales[:, b_cols],
-                    rhs=w_codes[:, g, k, :].bitcast(FP8X4),
-                    rhs_scale=w_scales[:, g, k, :],
-                    start=(g == 0 and k == 0),
-                    stop=(g == HALVES - 1 and k == BASES - 1),
-                )
+            nc.tensor.matmul_mx(
+                out=acc[:],
+                lhsT=w_codes[:, g, k, :].bitcast(FP8X4),
+                lhsT_scale=w_scales[:, g, k, :],
+                rhs=b_codes[:].bitcast(FP8X4),
+                rhs_scale=b_scales[:],
+                start=(g == 0 and k == 0),
+                stop=(g == HALVES - 1 and k == BASES - 1),
+            )
 
         def new_sums():
-            return [acc_psum.tile([P, OUTPUTS], F32, name="acc%d" % m) for m in range(ROW_TILES)]
+            return acc_psum.tile([P, ROWS], F32, name="acc")
 
-        def store_result(r, acc):
-            result = result_pool.tile([P, ROW_TILES, OUTPUTS], F32, name="result")
+        def copy_sums(acc):
+            sums = result_pool.tile([P, ROWS], F32, name="sums")
+            nc.scalar.copy(out=sums[:], in_=acc[:])
+            return sums
+
+        def store_result(r, sums):
+            flipped = sum_psum.tile([P, ROW_TILES, OUTPUTS], F32, name="sum")
             for m in range(ROW_TILES):
-                nc.scalar.copy(out=result[:, m, :], in_=acc[m][:])
+                nc.tensor.transpose(flipped[:, m, :], sums[:, m * P : (m + 1) * P], ident_f32[:])
+            result = result_pool.tile([P, ROW_TILES, OUTPUTS], F32, name="result")
+            nc.scalar.copy(out=result[:], in_=flipped[:])
             nc.sync.dma_start(
                 out=out[r * ROWS : (r + 1) * ROWS, :].rearrange("(m p) o -> p m o", p=P),
                 in_=result[:],
             )
 
         c = spline_constants(nc, consts, knots)
-        x_tiles = load_rows(0)
+        x_sb = load_chunk(0, 0)
         cp_tiles = [load_points(g) for g in range(HALVES)]
+        x_next = load_chunk(0, 1)
         ident = consts.tile([P, P], BF16)
         make_identity(nc, ident[:])
+        ident_f32 = consts.tile([P, P], F32)
+        make_identity(nc, ident_f32[:])
+        third_ident = consts.tile([P, P], F32)
+        nc.vector.tensor_scalar_mul(
+            out=third_ident[:], in0=ident_f32[:], scalar1=c["third_w"][:, 1:2]
+        )
 
-        v = copy_values(flip_values(x_tiles, 0), [nc.scalar.copy] * 2)
+        v = copy_values(flip_values(x_sb))
         square = {4: make_square(v, 4), 5: make_square(v, 5)}
         first = {i: new_first(i) for i in P_ONLY}
         for i in P_ONLY[1:]:
             clamp_distance(first[i], v, i)
         for i in P_ONLY:
-            log_distance(first[i], v, i)
+            log_distance(first[i], v, i, clamp_distance)
         cube = {4: signed_cube(v, 4, square[4])}
         square[6] = make_square(v, 6)
         for i in P_ONLY:
             cube_distance(first[i], i)
-        grouped = None
+        copied = None
         for g in range(HALVES):
             for k in range(0, BASES, 2):
                 w_grouped = flip_weights(cp_tiles[g], k)
-                if grouped:
-                    quantise_weights(*grouped)
-                grouped = (w_grouped, g, k)
-        quantise_weights(*grouped)
-        banks = flip_values(x_tiles, 1)
+                if copied:
+                    quantise_weights(*copied)
+                copied = (w_grouped, g, k)
+        quantise_weights(*copied)
+        flipped = flip_values(x_next)
 
         acc = new_sums()
         waiting = []
+        unjoined = []
 
         def quantise_waiting():
             if waiting:
                 multiply(*waiting.pop())
 
-        def join_last(three, edge, g, acc):
-            waiting.append((join(three, edge, ALU.min), 9, g, acc))
-
-        last = None
+        def join_unjoined():
+            joined = []
+            for one, other, op, k, g, acc in unjoined:
+                if len(joined) == 2:
+                    multiply(*joined.pop(0))
+                    multiply(*joined.pop(0))
+                joined.append((join(one, other, op), k, g, acc))
+            waiting.extend(joined)
 
         for r in range(ROUNDS):
             for g in range(HALVES):
                 final = r == ROUNDS - 1 and g == HALVES - 1
-                by_scalar = Q_ONLY if final else (13,) if r == 0 and g == 0 else (3, 11, 12, 13)
+                by_scalar = (10,) if final else () if r == 0 and g == 0 else (2,) if g else ()
+                def clamp_of(n):
+                    if n in ON_GPSIMD:
+                        return clamp_on_gpsimd
+                    return clamp_on_scalar if n in by_scalar else clamp_distance
+
                 p_cube = dict(first)
                 q_cube = new_last()
                 cube = {4: cube[4]}
@@ -430,6 +561,9 @@ def tile_kanlayer_kernel(tc, x, knots, control_points, out):
                         cube[5] = signed_cube(v, 5, square[5])
                         cube[6] = signed_cube(v, 6, square[6])
                         p_cube[5] = make_p(cube[5], 5)
+                        turned = [turn_one(p_cube[2], 0)]
+                        added = [turn_first_sum(p_cube, 0)]
+                        turned.append(turn_one(p_cube[2], 1))
                     elif i == 5:
                         p_cube[6] = make_p(cube[6], 6)
                         q_cube[6] = make_q(cube[6], 6)
@@ -439,47 +573,56 @@ def tile_kanlayer_kernel(tc, x, knots, control_points, out):
                         q_cube[i + 1] = make_q(cube[i + 1], i + 1)
                     elif not final:
                         cube[4] = signed_cube(v_after, 4, square[4])
-                    quantise_waiting()
-                    if i == 4 and last:
-                        join_last(*last)
-
-                    if i == 4 and not final:
-                        v_after = copy_values(banks, [nc.scalar.copy] * 2)
-                    knots = (10, 11, 12) if i == 4 else (13,) if i == 5 else ()
-                    for n in knots:
-                        (clamp_on_scalar if n in by_scalar else clamp_distance)(q_cube[n], v, n)
                     if i == 4:
+                        join_unjoined()
+                    elif i > 5:
+                        quantise_waiting()
+
+                    if i == 4:
+                        if not final:
+                            v_after = copy_values(flipped)
+                        for n in ON_GPSIMD:
+                            clamp_of(n)(q_cube[n], v, n)
+                        if clamp_of(10) is clamp_on_scalar:
+                            clamp_of(10)(q_cube[10], v, 10)
                         q_cube[5] = make_q(cube[5], 5)
+                    if i == 6 and g == 0 and r > 0:
+                        store_result(r - 1, sums)
+                    if i == 5:
+                        log_distance(q_cube[10], v, 10, clamp_of(10))
                     if i == 5 and not final:
                         first = {n: new_first(n) for n in P_ONLY}
-                        log_distance(first[0], v_after, 0)
-                    for n in knots:
-                        log_distance(q_cube[n], v, n, clamp=n in by_scalar)
+                        log_distance(first[0], v_after, 0, None)
+                    if 5 <= i <= 7:
+                        log_distance(q_cube[i + 6], v, i + 6, clamp_of(i + 6))
                     if 6 <= i <= 8 and not final:
-                        log_distance(first[i - 5], v_after, i - 5, clamp=i - 5 in by_scalar)
+                        log_distance(first[i - 5], v_after, i - 5, clamp_of(i - 5))
                     if 5 <= i <= 7 and not final:
-                        n = i - 4
-                        (clamp_on_scalar if n in by_scalar else clamp_distance)(
-                            first[n], v_after, n
-                        )
+                        clamp_of(i - 4)(first[i - 4], v_after, i - 4)
+                    if i == 5:
+                        quantise_waiting()
                     if i == 8:
-                        cube_distance(q_cube[10], 10)
-                    if i == 9:
-                        for n in Q_ONLY[1:]:
+                        for n in Q_ONLY:
                             cube_distance(q_cube[n], n)
 
-                    if i == 5 and g == 0 and r < ROUNDS - 1:
-                        x_tiles = load_rows(r + 1)
+                    if i == 5 and r < ROUNDS - 1:
+                        x_next = load_chunk(r + 1, g)
 
                     if i == 4:
-                        two = combine(p_cube[0], p_cube[1], c["left_w"][:, 0:1], p_cube[0])
+                        left[1], left[2], three = new_left(), new_left(), new_right()
+                        for m in range(ROW_TILES):
+                            use_second(m, turned.pop(0), p_cube, left)
+                            if m + 1 < ROW_TILES:
+                                added.append(turn_first_sum(p_cube, m + 1))
+                            use_first_sum(m, added.pop(0), p_cube, three)
+                            if m + 2 < ROW_TILES:
+                                turned.append(turn_one(p_cube[2], m + 2))
                         quantise_waiting()
                         if g == 0 and r > 0:
-                            store_result(r - 1, acc)
+                            sums = copy_sums(acc)
                             acc = new_sums()
-                        left[1] = left_side(1, p_cube)
-                        three = combine(new_right(), p_cube[2], c["third_w"][:, 0:1], two)
-                        left[2] = left_side(2, p_cube)
+                        if clamp_of(10) is clamp_distance:
+                            clamp_of(10)(q_cube[10], v, 10)
                         left[3] = left_side(3, p_cube)
                         waiting.append((join(three, q_cube[4], ALU.min), 0, g, acc))
                     else:
@@ -492,22 +635,36 @@ def tile_kanlayer_kernel(tc, x, knots, control_points, out):
                         for n in P_ONLY:
                             cube_distance(first[n], n)
 
-                for k in (6, 7):
-                    right = right_side(k, q_cube, cube)
-                    quantise_waiting()
-                    waiting.append((join(left[k], right, ALU.max), k, g, acc))
-                two = combine(q_cube[13], q_cube[12], c["right_w"][:, 9:10], q_cube[13])
-                right = right_side(8, q_cube, cube)
-                quantise_waiting()
-                three = combine(new_right(), q_cube[11], c["third_w"][:, 1:2], two)
-                waiting.append((join(left[8], right, ALU.max), 8, g, acc))
-                last = (three, make_edge(cube[9]), g, acc)
+                turned = [turn_one(q_cube[11], 0)]
+                added = [turn_last_sum(q_cube, 0)]
+                turned.append(turn_one(q_cube[11], 1))
+                right = right_side(6, q_cube, cube)
+                sixth = right
+                right = {7: new_right(), 8: new_right()}
+                for m in range(ROW_TILES):
+                    use_eleventh(m, turned.pop(0), q_cube, right)
+                    if m + 1 < ROW_TILES:
+                        added.append(turn_last_sum(q_cube, m + 1))
+                    if m == 0:
+                        joined = (join(left[6], sixth, ALU.max), 6, g, acc)
+                        quantise_waiting()
+                        waiting.append(joined)
+                        three = new_right()
+                    use_last_sum(m, added.pop(0), q_cube, three)
+                    if m + 2 < ROW_TILES:
+                        turned.append(turn_one(q_cube[11], m + 2))
+                    if m == 2:
+                        quantise_waiting()
+                unjoined = [
+                    (left[7], right[7], ALU.max, 7, g, acc),
+                    (left[8], right[8], ALU.max, 8, g, acc),
+                    (three, make_edge(cube[9]), ALU.min, 9, g, acc),
+                ]
                 if not final:
                     v = v_after
                     if r < ROUNDS - 1:
-                        banks = flip_values(x_tiles, g)
+                        flipped = flip_values(x_next)
 
+        join_unjoined()
         quantise_waiting()
-        join_last(*last)
-        quantise_waiting()
-        store_result(ROUNDS - 1, acc)
+        store_result(ROUNDS - 1, copy_sums(acc))

from contextlib import ExitStack

import concourse.mybir as mybir
from concourse.masks import make_identity

F32 = mybir.dt.float32
BF16 = mybir.dt.bfloat16
U32 = mybir.dt.uint32
U8 = mybir.dt.uint8
FP8X4 = mybir.dt.float8_e4m3fn_x4
ALU = mybir.AluOpType
ACT = mybir.ActivationFunctionType

P = 128
PACK = 4
BATCH = 2048
FEATURES = 1024
OUTPUTS = 128
KNOTS = 14
POINTS = 13
BASES = 10
PASS = P * PACK
HALVES = FEATURES // PASS
ROWS = 512
ROW_TILES = ROWS // P
ROUNDS = BATCH // ROWS
CHUNK = ROWS * PACK
BOUND = 2.0**100
STEP = 2.0**-24
TINY = 2.0**-60

P_ONLY = (0, 1, 2, 3)
BOTH = (4, 5, 6, 7, 8, 9)
Q_ONLY = (10, 11, 12, 13)
ON_GPSIMD = (10, 11, 12, 13)
BY_ROWS = (0, 2, 11, 13)

FLOPS = 2 * BATCH * BASES * FEATURES * OUTPUTS


def feature_columns(n):
    g, t = divmod(n, PACK)
    return slice(g * PASS + t, (g + 1) * PASS, PACK)


def spline_constants(nc, pool, knots):
    knots_bf = pool.tile([P, KNOTS], BF16)
    nc.sync.dma_start(out=knots_bf[:], in_=knots.partition_broadcast(P))
    t = pool.tile([P, KNOTS], F32)
    nc.vector.tensor_copy(out=t[:], in_=knots_bf[:])
    neg_t = pool.tile([P, KNOTS], F32)
    nc.vector.tensor_scalar_mul(out=neg_t[:], in0=t[:], scalar1=-1.0)
    first_bias = pool.tile([P, 1], F32)
    nc.vector.tensor_scalar_add(out=first_bias[:], in0=neg_t[:, 0:1], scalar1=TINY)

    d1 = pool.tile([P, KNOTS - 1], F32)
    d2 = pool.tile([P, KNOTS - 2], F32)
    d3 = pool.tile([P, KNOTS - 3], F32)
    d4 = pool.tile([P, KNOTS - 4], F32)
    for step, diff in ((1, d1), (2, d2), (3, d3), (4, d4)):
        nc.vector.tensor_sub(out=diff[:], in0=t[:, step:KNOTS], in1=t[:, 0 : KNOTS - step])

    cubes = KNOTS - 3
    p_prod = pool.tile([P, cubes], F32)
    nc.vector.tensor_mul(out=p_prod[:], in0=d1[:, 0:cubes], in1=d2[:, 0:cubes])
    nc.vector.tensor_mul(out=p_prod[:], in0=p_prod[:], in1=d3[:, 0:cubes])
    p_factor = pool.tile([P, cubes], F32)
    nc.vector.reciprocal(out=p_factor[:], in_=p_prod[:])
    q_prod = pool.tile([P, cubes], F32)
    nc.vector.tensor_mul(out=q_prod[:], in0=d1[:, 2 : 2 + cubes], in1=d2[:, 1 : 1 + cubes])
    nc.vector.tensor_mul(out=q_prod[:], in0=q_prod[:], in1=d3[:, 0:cubes])
    q_factor = pool.tile([P, cubes], F32)
    nc.vector.reciprocal(out=q_factor[:], in_=q_prod[:])
    q_log = pool.tile([P, cubes], F32)
    nc.scalar.activation(out=q_log[:], in_=q_factor[:], func=ACT.Ln)

    d1_recip = pool.tile([P, KNOTS - 1], F32)
    nc.vector.reciprocal(out=d1_recip[:], in_=d1[:])
    neg_d4 = pool.tile([P, BASES], F32)
    nc.vector.tensor_scalar_mul(out=neg_d4[:], in0=d4[:], scalar1=-1.0)
    left_w = pool.tile([P, BASES], F32)
    nc.vector.tensor_mul(out=left_w[:], in0=neg_d4[:], in1=d1_recip[:, 0:BASES])
    right_w = pool.tile([P, BASES], F32)
    nc.vector.tensor_mul(out=right_w[:], in0=neg_d4[:], in1=d1_recip[:, 3 : 3 + BASES])

    third_w = pool.tile([P, 2], F32)
    third_den = pool.tile([P, 2], F32)
    for n, (k, i, j, m) in enumerate(((0, 2, 0, 1), (9, 8, 11, 11))):
        col = slice(n, n + 1)
        nc.vector.tensor_mul(out=third_w[:, col], in0=d4[:, k : k + 1], in1=d3[:, i : i + 1])
        nc.vector.tensor_mul(out=third_den[:, col], in0=d2[:, j : j + 1], in1=d1[:, m : m + 1])
    third_recip = pool.tile([P, 2], F32)
    nc.vector.reciprocal(out=third_recip[:], in_=third_den[:])
    nc.vector.tensor_mul(out=third_w[:], in0=third_w[:], in1=third_recip[:])

    norm = pool.tile([P, BASES], F32)
    nc.vector.memset(norm[:], 1.0)
    nc.vector.tensor_copy(out=norm[:, 2:3], in_=third_w[:, 0:1])
    nc.vector.tensor_scalar_mul(out=norm[:, 3:BASES], in0=left_w[:, 2 : BASES - 1], scalar1=-1.0)
    left_scale = pool.tile([P, BASES], F32)
    nc.vector.reciprocal(out=left_scale[:], in_=norm[:])
    second_w = pool.tile([P, 1], F32)
    nc.vector.tensor_mul(out=second_w[:], in0=left_w[:, 1:2], in1=left_scale[:, 2:3])
    p_normed = pool.tile([P, BASES], F32)
    nc.vector.tensor_mul(out=p_normed[:], in0=p_factor[:, 0:BASES], in1=norm[:])
    p_log = pool.tile([P, BASES], F32)
    nc.scalar.activation(out=p_log[:], in_=p_normed[:], func=ACT.Ln)

    both = len(BOTH)
    factor = pool.tile([P, both], F32)
    nc.vector.tensor_copy(out=factor[:], in_=p_normed[:, 4 : 4 + both])
    nc.vector.tensor_mul(out=factor[:, 0:1], in0=q_factor[:, 1:2], in1=right_w[:, 1:2])
    nc.vector.tensor_scalar_mul(out=factor[:, 0:1], in0=factor[:, 0:1], scalar1=-1.0)
    half = pool.tile([P, both], F32)
    nc.gpsimd.memset(half[:], 0.5)
    root = pool.tile([P, both], F32)
    nc.gpsimd.tensor_tensor(out=root[:], in0=factor[:], in1=half[:], op=ALU.pow)
    root_bias = pool.tile([P, both], F32)
    nc.vector.tensor_mul(out=root_bias[:], in0=root[:], in1=neg_t[:, 4 : 4 + both])
    recip = pool.tile([P, both], F32)
    nc.vector.reciprocal(out=recip[:], in_=factor[:])

    p_side = pool.tile([P, 1], F32)
    nc.vector.tensor_mul(out=p_side[:], in0=p_normed[:, 4:5], in1=recip[:, 0:1])
    q_side = pool.tile([P, both], F32)
    nc.vector.tensor_scalar_mul(out=q_side[:], in0=q_factor[:, 1 : 1 + both], scalar1=-1.0)
    nc.vector.tensor_mul(out=q_side[:], in0=q_side[:], in1=recip[:])
    tiny = pool.tile([P, 1], F32)
    nc.vector.memset(tiny[:], TINY)
    below_t = pool.tile([P, KNOTS], F32)
    nc.vector.tensor_scalar_add(out=below_t[:], in0=t[:], scalar1=-STEP)
    return {
        "t": t,
        "below_t": below_t,
        "neg_t": neg_t,
        "first_bias": first_bias,
        "tiny": tiny,
        "p_log": p_log,
        "q_log": q_log,
        "left_w": left_w,
        "right_w": right_w,
        "third_w": third_w,
        "left_scale": left_scale,
        "second_w": second_w,
        "root": root,
        "root_bias": root_bias,
        "p_side": p_side,
        "q_side": q_side,
    }


def tile_kanlayer_kernel(tc, x, knots, control_points, out):
    nc = tc.nc
    with ExitStack() as ctx:
        consts = ctx.enter_context(tc.tile_pool(name="consts", bufs=1))
        weights = ctx.enter_context(tc.tile_pool(name="weights", bufs=1))
        x_pool = ctx.enter_context(tc.tile_pool(name="x_pool", bufs=2))
        v_pool = ctx.enter_context(tc.tile_pool(name="v_pool", bufs=2))
        right_pool = ctx.enter_context(tc.tile_pool(name="right_pool", bufs=3))
        result_pool = ctx.enter_context(tc.tile_pool(name="result_pool", bufs=1))
        single_pool = ctx.enter_context(tc.tile_pool(name="single_pool", bufs=1))
        square_pool = ctx.enter_context(tc.tile_pool(name="square_pool", bufs=2))
        cube_pool = ctx.enter_context(tc.tile_pool(name="cube_pool", bufs=4))
        p_pool = ctx.enter_context(tc.tile_pool(name="p_pool", bufs=2))
        q_pool = ctx.enter_context(tc.tile_pool(name="q_pool", bufs=3))
        edge_pool = ctx.enter_context(tc.tile_pool(name="edge_pool", bufs=1))
        left_pool = ctx.enter_context(tc.tile_pool(name="left_pool", bufs=5))
        mx_pool = ctx.enter_context(tc.tile_pool(name="mx_pool", bufs=2))
        flip_psum = ctx.enter_context(tc.psum_pool(name="flip_psum", bufs=4))
        sum_psum = ctx.enter_context(tc.psum_pool(name="sum_psum", bufs=3))
        acc_psum = ctx.enter_context(tc.psum_pool(name="acc_psum", bufs=1))
        ctx.enter_context(
            tc.manual_schedule(engines={mybir.EngineType.Activation, mybir.EngineType.DVE})
        )

        def load_chunk(r, g):
            x_sb = x_pool.tile([P, ROW_TILES, PASS], BF16, name="x_sb")
            for m in range(ROW_TILES):
                row = r * ROWS + m * P
                nc.sync.dma_start(
                    out=x_sb[:, m, :], in_=x[row : row + P, g * PASS : (g + 1) * PASS]
                )
            return x_sb

        def flip_values(x_sb):
            banks = []
            for pair in range(2):
                bank = flip_psum.tile([P, PACK, 2 * P], BF16, name="flip")
                for n in range(2):
                    for t in range(PACK):
                        nc.tensor.transpose(
                            bank[:, t, n * P : (n + 1) * P],
                            x_sb[:, 2 * pair + n, feature_columns(t)],
                            ident[:],
                        )
                banks.append(bank[:].rearrange("p t b -> p b t"))
            return banks, x_sb[:].rearrange("p m (q t) -> p m t q", t=PACK)

        def copy_values(flipped):
            banks, by_rows = flipped
            v = v_pool.tile([P, ROWS, PACK], BF16, name="v")
            for n, bank in enumerate(banks):
                nc.scalar.copy(out=v[:, 2 * n * P : 2 * (n + 1) * P, :], in_=bank)
            return v[:].rearrange("p b t -> p (b t)"), banks, by_rows

        w_codes = weights.tile([P, HALVES, BASES, OUTPUTS], U32, align_bytes=64)
        w_scales = weights.tile([P, HALVES, BASES, OUTPUTS], U8, align_bytes=64)

        def load_points(g):
            cp_sb = single_pool.tile([P, PASS, POINTS], BF16, name="last%d" % g)
            nc.sync.dma_start(
                out=cp_sb[:], in_=control_points[:, g * PASS : (g + 1) * PASS, :]
            )
            return cp_sb

        def flip_weights(cp_sb, k):
            w_flip = flip_psum.tile([P, 2, PACK, P], BF16, name="flip")
            for n in range(2):
                for t in range(PACK):
                    nc.tensor.transpose(
                        w_flip[:, n, t, :], cp_sb[:, feature_columns(t), k + n], ident[:]
                    )
            w_grouped = right_pool.tile(
                [P, 2, OUTPUTS, PACK], BF16, name="right", align_bytes=64
            )
            nc.vector.tensor_copy(out=w_grouped[:], in_=w_flip[:].rearrange("p n t o -> p n o t"))
            return w_grouped

        def quantise_weights(w_grouped, g, k):
            nc.vector.quantize_mx(
                out=w_codes[:, g, k : k + 2, :].rearrange("p n o -> p (n o)").bitcast(FP8X4),
                scales=w_scales[:, g, k : k + 2, :].rearrange("p n o -> p (n o)"),
                in_=w_grouped[:].rearrange("p n o t -> p (n o t)"),
            )

        def operands(dist, v, i):
            if i in BY_ROWS:
                return dist.rearrange("p (m t q) -> p m t q", m=ROW_TILES, t=PACK), v[2]
            return dist, v[0]

        def clamp_on_gpsimd(dist, v, i):
            out, values = operands(dist, v, i)
            nc.gpsimd.tensor_scalar(
                out=out,
                in0=values,
                scalar1=c["below_t"][:, i : i + 1],
                scalar2=-BOUND,
                op0=ALU.min,
                op1=ALU.max,
            )

        def clamp_distance(dist, v, i):
            on_right = i in P_ONLY
            out, values = operands(dist, v, i)
            nc.vector.tensor_scalar(
                out=out,
                in0=values,
                scalar1=c["t"][:, i : i + 1],
                scalar2=TINY if on_right else -TINY,
                op0=ALU.subtract,
                op1=ALU.max if on_right else ALU.min,
            )

        def clamp_on_scalar(dist, v, i):
            sign, bias = (1.0, c["neg_t"]) if i in P_ONLY else (-1.0, c["t"])
            out, values = operands(dist, v, i)
            nc.scalar.activation(
                out=out, in_=values, func=ACT.Relu, scale=sign, bias=bias[:, i : i + 1]
            )

        def log_distance(dist, v, i, clamp):
            if i == 0:
                out, values = operands(dist, v, i)
                nc.scalar.activation(out=out, in_=values, func=ACT.Ln, bias=c["first_bias"][:])
            elif clamp is clamp_on_gpsimd:
                nc.scalar.activation(
                    out=dist, in_=dist, func=ACT.Ln, scale=-1.0, bias=c["t"][:, i : i + 1]
                )
            elif clamp is clamp_on_scalar:
                nc.scalar.activation(out=dist, in_=dist, func=ACT.Ln, bias=c["tiny"][:])
            else:
                sign = 1.0 if i in P_ONLY else -1.0
                nc.scalar.activation(out=dist, in_=dist, func=ACT.Ln, scale=sign)

        def cube_distance(dist, i):
            factor = c["p_log"][:, i : i + 1] if i in P_ONLY else c["q_log"][:, i - 3 : i - 2]
            nc.scalar.activation(out=dist, in_=dist, func=ACT.Exp, scale=3.0, bias=factor)

        def new_first(i):
            tile = single_pool.tile([P, CHUNK], F32, name="first%d" % i)
            return tile[:]

        def new_last():
            pairs = [single_pool.tile([P, 2, CHUNK], F32, name="last%d" % n) for n in range(2)]
            return {i: pairs[(i - 10) // 2][:, i % 2, :] for i in Q_ONLY}

        def make_square(v, i):
            square = square_pool.tile([P, CHUNK], F32, name="square")
            nc.scalar.activation(
                out=square[:],
                in_=v[0],
                func=ACT.Square,
                bias=c["root_bias"][:, i - 4 : i - 3],
                scale=c["root"][:, i - 4 : i - 3],
            )
            return square

        def bank_part(tile, n):
            half = CHUNK // 2
            return tile[:, n * half : (n + 1) * half].rearrange("p (b t) -> p b t", t=PACK)

        def signed_cube(v, i, square):
            cube = cube_pool.tile([P, CHUNK], F32, name="cube")
            for n, bank in enumerate(v[1]):
                nc.vector.scalar_tensor_tensor(
                    out=bank_part(cube, n),
                    in0=bank,
                    scalar=c["t"][:, i : i + 1],
                    in1=bank_part(square, n),
                    op0=ALU.subtract,
                    op1=ALU.mult,
                )
            return cube

        def relu_of(cube, scale, tile):
            nc.scalar.activation(out=tile[:], in_=cube[:], func=ACT.Relu, scale=scale)
            return tile[:]

        def make_p(cube, i):
            side = p_pool.tile([P, CHUNK], F32, name="p_cube")
            if i == 4:
                return relu_of(cube, c["p_side"][:], side)
            nc.gpsimd.tensor_scalar(
                out=side[:],
                in0=cube[:],
                scalar1=BOUND,
                scalar2=0.0,
                op0=ALU.min,
                op1=ALU.max,
            )
            return side[:]

        def make_edge(cube):
            edge = left_pool.tile([P, CHUNK], BF16, name="left")
            return relu_of(cube, c["left_scale"][:, 9:10], edge)

        def make_q(cube, i):
            if i == 4:
                side = edge_pool.tile([P, CHUNK], BF16, name="edge")
            else:
                side = q_pool.tile([P, CHUNK], F32, name="q_cube")
            return relu_of(cube, c["q_side"][:, i - 4 : i - 3], side)

        def combine(out, in0, weight, in1):
            nc.vector.scalar_tensor_tensor(
                out=out, in0=in0, scalar=weight, in1=in1, op0=ALU.mult, op1=ALU.add
            )
            return out

        def difference(out, in0, weight, in1):
            nc.vector.scalar_tensor_tensor(
                out=out, in0=in0, scalar=weight, in1=in1, op0=ALU.mult, op1=ALU.subtract
            )
            return out

        def new_left():
            left = left_pool.tile([P, CHUNK], BF16, name="left")
            return left[:]

        def new_right():
            right = right_pool.tile([P, CHUNK], BF16, name="right", align_bytes=64)
            return right[:]

        def left_side(k, p_cube):
            return difference(new_left(), p_cube[k], c["left_scale"][:, k : k + 1], p_cube[k + 1])

        def row_tile_columns(m, t):
            return slice((m * PACK + t) * P, (m * PACK + t + 1) * P)

        def turn(cube, m, bank, t, start=True, stop=True):
            nc.tensor.matmul(
                bank[:, t, :],
                lhsT=cube[:, row_tile_columns(m, t)],
                rhs=ident_f32[:],
                is_transpose=True,
                start=start,
                stop=stop,
            )

        def new_bank():
            bank = sum_psum.tile([P, PACK, P], F32, name="sum")
            return bank

        def turn_one(cube, m):
            bank = new_bank()
            for t in range(PACK):
                turn(cube, m, bank, t)
            return bank[:].rearrange("p t b -> p b t")

        def turn_first_sum(p_cube, m):
            bank = new_bank()
            for t in range(PACK):
                turn(p_cube[2], m, bank, t, stop=False)
                turn(p_cube[0], m, bank, t, start=False)
            return bank[:].rearrange("p t b -> p b t")

        def turn_last_sum(q_cube, m):
            bank = new_bank()
            for t in range(PACK):
                nc.tensor.matmul(
                    bank[:, t, :],
                    lhsT=q_cube[11][:, row_tile_columns(m, t)],
                    rhs=third_ident[:],
                    start=True,
                    stop=False,
                )
                turn(q_cube[13], m, bank, t, start=False)
            return bank[:].rearrange("p t b -> p b t")

        def row_tile(row, m):
            return row[:, m * PACK * P : (m + 1) * PACK * P].rearrange("p (b t) -> p b t", t=PACK)

        def use_second(m, bank, p_cube, left):
            combine(row_tile(left[1], m), bank, c["second_w"][:], row_tile(p_cube[1], m))
            difference(
                row_tile(left[2], m), bank, c["left_scale"][:, 2:3], row_tile(p_cube[3], m)
            )

        def use_first_sum(m, bank, p_cube, three):
            combine(row_tile(three, m), row_tile(p_cube[1], m), c["left_w"][:, 0:1], bank)

        def use_eleventh(m, bank, q_cube, right):
            combine(row_tile(right[7], m), row_tile(q_cube[10], m), c["right_w"][:, 7:8], bank)
            combine(row_tile(right[8], m), bank, c["right_w"][:, 8:9], row_tile(q_cube[12], m))

        def use_last_sum(m, bank, q_cube, three):
            combine(row_tile(three, m), row_tile(q_cube[12], m), c["right_w"][:, 9:10], bank)

        def right_side(k, q_cube, cube):
            if k == 1:
                right = new_right()
                nc.vector.scalar_tensor_tensor(
                    out=right, in0=cube[4][:], scalar=0.0, in1=q_cube[5], op0=ALU.min, op1=ALU.add
                )
                return right
            return combine(new_right(), q_cube[k + 3], c["right_w"][:, k : k + 1], q_cube[k + 4])

        def join(one, other, op):
            basis = mx_pool.tile([P, CHUNK], BF16, name="basis", align_bytes=64)
            nc.vector.tensor_tensor(out=basis[:], in0=one, in1=other, op=op)
            return basis

        def multiply(basis, k, g, acc):
            b_codes = mx_pool.tile([P, ROWS], U32, name="b_codes", align_bytes=64)
            b_scales = mx_pool.tile([P, ROWS], U8, name="b_scales", align_bytes=64)
            nc.vector.quantize_mx(
                out=b_codes[:].bitcast(FP8X4), scales=b_scales[:], in_=basis[:]
            )
            nc.tensor.matmul_mx(
                out=acc[:],
                lhsT=w_codes[:, g, k, :].bitcast(FP8X4),
                lhsT_scale=w_scales[:, g, k, :],
                rhs=b_codes[:].bitcast(FP8X4),
                rhs_scale=b_scales[:],
                start=(g == 0 and k == 0),
                stop=(g == HALVES - 1 and k == BASES - 1),
            )

        def new_sums():
            return acc_psum.tile([P, ROWS], F32, name="acc")

        def copy_sums(acc):
            sums = result_pool.tile([P, ROWS], F32, name="sums")
            nc.scalar.copy(out=sums[:], in_=acc[:])
            return sums

        def store_result(r, sums):
            flipped = sum_psum.tile([P, ROW_TILES, OUTPUTS], F32, name="sum")
            for m in range(ROW_TILES):
                nc.tensor.transpose(flipped[:, m, :], sums[:, m * P : (m + 1) * P], ident_f32[:])
            result = result_pool.tile([P, ROW_TILES, OUTPUTS], F32, name="result")
            nc.scalar.copy(out=result[:], in_=flipped[:])
            nc.sync.dma_start(
                out=out[r * ROWS : (r + 1) * ROWS, :].rearrange("(m p) o -> p m o", p=P),
                in_=result[:],
            )

        c = spline_constants(nc, consts, knots)
        x_sb = load_chunk(0, 0)
        cp_tiles = [load_points(g) for g in range(HALVES)]
        x_next = load_chunk(0, 1)
        ident = consts.tile([P, P], BF16)
        make_identity(nc, ident[:])
        ident_f32 = consts.tile([P, P], F32)
        make_identity(nc, ident_f32[:])
        third_ident = consts.tile([P, P], F32)
        nc.vector.tensor_scalar_mul(
            out=third_ident[:], in0=ident_f32[:], scalar1=c["third_w"][:, 1:2]
        )

        v = copy_values(flip_values(x_sb))
        square = {4: make_square(v, 4), 5: make_square(v, 5)}
        first = {i: new_first(i) for i in P_ONLY}
        for i in P_ONLY[1:]:
            clamp_distance(first[i], v, i)
        for i in P_ONLY:
            log_distance(first[i], v, i, clamp_distance)
        cube = {4: signed_cube(v, 4, square[4])}
        square[6] = make_square(v, 6)
        for i in P_ONLY:
            cube_distance(first[i], i)
        copied = None
        for g in range(HALVES):
            for k in range(0, BASES, 2):
                w_grouped = flip_weights(cp_tiles[g], k)
                if copied:
                    quantise_weights(*copied)
                copied = (w_grouped, g, k)
        quantise_weights(*copied)
        flipped = flip_values(x_next)

        acc = new_sums()
        waiting = []
        unjoined = []

        def quantise_waiting():
            if waiting:
                multiply(*waiting.pop())

        def join_unjoined():
            joined = []
            for one, other, op, k, g, acc in unjoined:
                if len(joined) == 2:
                    multiply(*joined.pop(0))
                    multiply(*joined.pop(0))
                joined.append((join(one, other, op), k, g, acc))
            waiting.extend(joined)

        for r in range(ROUNDS):
            for g in range(HALVES):
                final = r == ROUNDS - 1 and g == HALVES - 1
                by_scalar = (10,) if final else () if r == 0 and g == 0 else (2,) if g else ()
                def clamp_of(n):
                    if n in ON_GPSIMD:
                        return clamp_on_gpsimd
                    return clamp_on_scalar if n in by_scalar else clamp_distance

                p_cube = dict(first)
                q_cube = new_last()
                cube = {4: cube[4]}
                left = {}

                for i in BOTH:
                    if 5 <= i <= 7:
                        square[i + 2] = make_square(v, i + 2)
                    elif i >= 8 and not final:
                        square[i - 4] = make_square(v_after, i - 4)
                    if i == 4:
                        p_cube[4] = make_p(cube[4], 4)
                        q_cube[4] = make_q(cube[4], 4)
                        cube[5] = signed_cube(v, 5, square[5])
                        cube[6] = signed_cube(v, 6, square[6])
                        p_cube[5] = make_p(cube[5], 5)
                        turned = [turn_one(p_cube[2], 0)]
                        added = [turn_first_sum(p_cube, 0)]
                        turned.append(turn_one(p_cube[2], 1))
                    elif i == 5:
                        p_cube[6] = make_p(cube[6], 6)
                        q_cube[6] = make_q(cube[6], 6)
                    elif i < BOTH[-1]:
                        cube[i + 1] = signed_cube(v, i + 1, square[i + 1])
                        p_cube[i + 1] = make_p(cube[i + 1], i + 1)
                        q_cube[i + 1] = make_q(cube[i + 1], i + 1)
                    elif not final:
                        cube[4] = signed_cube(v_after, 4, square[4])
                    if i == 4:
                        join_unjoined()
                    elif i > 5:
                        quantise_waiting()

                    if i == 4:
                        if not final:
                            v_after = copy_values(flipped)
                        for n in ON_GPSIMD:
                            clamp_of(n)(q_cube[n], v, n)
                        if clamp_of(10) is clamp_on_scalar:
                            clamp_of(10)(q_cube[10], v, 10)
                        q_cube[5] = make_q(cube[5], 5)
                    if i == 6 and g == 0 and r > 0:
                        store_result(r - 1, sums)
                    if i == 5:
                        log_distance(q_cube[10], v, 10, clamp_of(10))
                    if i == 5 and not final:
                        first = {n: new_first(n) for n in P_ONLY}
                        log_distance(first[0], v_after, 0, None)
                    if 5 <= i <= 7:
                        log_distance(q_cube[i + 6], v, i + 6, clamp_of(i + 6))
                    if 6 <= i <= 8 and not final:
                        log_distance(first[i - 5], v_after, i - 5, clamp_of(i - 5))
                    if 5 <= i <= 7 and not final:
                        clamp_of(i - 4)(first[i - 4], v_after, i - 4)
                    if i == 5:
                        quantise_waiting()
                    if i == 8:
                        for n in Q_ONLY:
                            cube_distance(q_cube[n], n)

                    if i == 5 and r < ROUNDS - 1:
                        x_next = load_chunk(r + 1, g)

                    if i == 4:
                        left[1], left[2], three = new_left(), new_left(), new_right()
                        for m in range(ROW_TILES):
                            use_second(m, turned.pop(0), p_cube, left)
                            if m + 1 < ROW_TILES:
                                added.append(turn_first_sum(p_cube, m + 1))
                            use_first_sum(m, added.pop(0), p_cube, three)
                            if m + 2 < ROW_TILES:
                                turned.append(turn_one(p_cube[2], m + 2))
                        quantise_waiting()
                        if g == 0 and r > 0:
                            sums = copy_sums(acc)
                            acc = new_sums()
                        if clamp_of(10) is clamp_distance:
                            clamp_of(10)(q_cube[10], v, 10)
                        left[3] = left_side(3, p_cube)
                        waiting.append((join(three, q_cube[4], ALU.min), 0, g, acc))
                    else:
                        k = i - 4
                        right = right_side(k, q_cube, cube)
                        left[i - 1] = left_side(i - 1, p_cube)
                        waiting.append((join(left[k], right, ALU.max), k, g, acc))
                    if i == 9 and not final:
                        square[6] = make_square(v_after, 6)
                        for n in P_ONLY:
                            cube_distance(first[n], n)

                turned = [turn_one(q_cube[11], 0)]
                added = [turn_last_sum(q_cube, 0)]
                turned.append(turn_one(q_cube[11], 1))
                right = right_side(6, q_cube, cube)
                sixth = right
                right = {7: new_right(), 8: new_right()}
                for m in range(ROW_TILES):
                    use_eleventh(m, turned.pop(0), q_cube, right)
                    if m + 1 < ROW_TILES:
                        added.append(turn_last_sum(q_cube, m + 1))
                    if m == 0:
                        joined = (join(left[6], sixth, ALU.max), 6, g, acc)
                        quantise_waiting()
                        waiting.append(joined)
                        three = new_right()
                    use_last_sum(m, added.pop(0), q_cube, three)
                    if m + 2 < ROW_TILES:
                        turned.append(turn_one(q_cube[11], m + 2))
                    if m == 2:
                        quantise_waiting()
                unjoined = [
                    (left[7], right[7], ALU.max, 7, g, acc),
                    (left[8], right[8], ALU.max, 8, g, acc),
                    (three, make_edge(cube[9]), ALU.min, 9, g, acc),
                ]
                if not final:
                    v = v_after
                    if r < ROUNDS - 1:
                        flipped = flip_values(x_next)

        join_unjoined()
        quantise_waiting()
        store_result(ROUNDS - 1, copy_sums(acc))
